import numpy as np
import ml_dtypes


def mxq(x, axis, fmt="e4m3"):
    dtype, down = {"e4m3": (ml_dtypes.float8_e4m3fn, 7), "e5m2": (ml_dtypes.float8_e5m2, 14)}[fmt]
    v = np.moveaxis(np.asarray(x, np.float32).astype(ml_dtypes.bfloat16).astype(np.float64), axis, -1)
    blocks = v.reshape(v.shape[:-1] + (-1, 32))
    amax = np.abs(blocks).max(-1, keepdims=True)
    byte = np.maximum(np.where(amax > 0, np.frexp(amax)[1] - 1 + 127, 0) - down, 1)
    scale = np.exp2(byte - 127.0)
    codes = (blocks / scale).astype(np.float32).astype(dtype).astype(np.float64)
    return np.moveaxis((codes * scale).reshape(v.shape), -1, axis)


WIDE = False


def mx_kscale(k):
    if not WIDE:
        return np.ones(k)
    levels = np.array([18, -18])
    if k % 512:
        return np.exp2(np.random.permutation(np.resize(levels, k // 32))).repeat(32)
    a = np.empty((k // 512, 16))
    for p in range(k // 512):
        a[p, :8] = np.random.permutation(np.resize(levels, 8))
        for g in range(8):
            far = levels[np.abs(levels - a[p, g]) >= 10]
            a[p, g + 8] = far[np.random.randint(len(far))]
    return np.exp2(a.ravel()).repeat(32)


BF16 = ml_dtypes.bfloat16


def bf(x):
    return np.asarray(x, np.float32).astype(BF16)


def f64(x):
    return np.asarray(x).astype(np.float64)


B, T, V, C, K = 16, 4, 32, 512, 512


def setup_inputs():
    n = np.random.standard_normal
    s = mx_kscale(B * V)[::V].reshape(B, 1, 1, 1)
    u = mx_kscale(K)
    v = mx_kscale(K)
    x0 = bf(0.7 * n((B, 1, V, C)) + 0.7 * n((B, T, V, C)))
    A = bf(np.eye(V) + 0.1 * n((K, V, V)))
    lam = bf(0.25 + 0.1 * np.random.random(1))
    phi_w0 = bf(n((C, K)) / np.sqrt(C))
    phi_b = bf(0.3 * n(K))
    theta_w0 = bf(n((C, K)) / np.sqrt(C))
    theta_b = bf(0.3 * n(K))
    kappa_w0 = bf(n((K, K)) / np.sqrt(K))
    kappa_b = bf(0.3 * n(K))
    g = bf(4.0 * n((B, K, V, V)) * np.exp2(np.random.randint(-6, 1, (B, 1, V, 1))) / s * u[None, :, None, None])
    p = (f64(x0) @ f64(phi_w0) + f64(phi_b)).mean(axis=1)
    th = (f64(x0) @ f64(theta_w0) + f64(theta_b)).mean(axis=1)
    return {
        "x": bf(f64(x0) * s),
        "A": A,
        "lam": lam,
        "phi_w": bf(f64(phi_w0) / v),
        "phi_b": phi_b,
        "theta_w": bf(f64(theta_w0) / v),
        "theta_b": theta_b,
        "kappa_w": bf(f64(kappa_w0) * v[:, None] / u),
        "kappa_b": kappa_b,
        "p": np.asarray(p, np.float32),
        "th": np.asarray(th, np.float32),
        "grad_out": g,
    }


def reference(x, A, lam, phi_w, phi_b, theta_w, theta_b, kappa_w, kappa_b, p, th, grad_out):
    dz2 = f64(lam) * np.transpose(f64(grad_out), (0, 2, 3, 1)).reshape(B * V * V, K)
    dF = mxq(dz2, 1, "e5m2") @ mxq(f64(kappa_w), 1, "e4m3").T
    F = np.tanh(f64(p)[:, :, None, :] - f64(th)[:, None, :, :])
    dS = dF.reshape(B, V, V, K) * (1.0 - F * F)
    dp = dS.sum(axis=2).reshape(B * V, K) / T
    dt = -dS.sum(axis=1).reshape(B * V, K) / T
    dz1 = np.concatenate([dp, dt], axis=1)
    w = np.concatenate([f64(phi_w), f64(theta_w)], axis=1)
    dxr = mxq(dz1, 1, "e5m2") @ mxq(w, 1, "e4m3").T
    dx = np.repeat(dxr.reshape(B, 1, V, C), T, axis=1)
    xt = np.transpose(f64(x), (1, 0, 2, 3)).reshape(T, B * V, C)
    xq = mxq(xt, 1, "e4m3")
    dphi_w = (np.transpose(xq, (0, 2, 1)) @ mxq(dp, 0, "e5m2")).sum(axis=0)
    return dx, dphi_w

@@ -1,0 +1,441 @@
+from contextlib import ExitStack
+
+import concourse.mybir as mybir
+from concourse.masks import make_identity
+
+B, T, V, C, K = 16, 4, 32, 512, 512
+P = 128
+PACK = 4
+TOK = V * V
+HALF = 512
+N_UNITS = B * PACK
+FLOPS = 2 * B * TOK * K * K + 2 * (B * V) * (2 * K) * C + 2 * T * C * (B * V) * K
+BYTES = (
+    B * T * V * C * 2 + 3 * C * K * 2 + 2 * B * V * K * 4 + B * K * TOK * 2 + 2
+    + B * T * V * C * 4 + C * K * 4
+)
+
+F32 = mybir.dt.float32
+BF16 = mybir.dt.bfloat16
+U32 = mybir.dt.uint32
+U8 = mybir.dt.uint8
+E4 = mybir.dt.float8_e4m3fn_x4
+E5 = mybir.dt.float8_e5m2_x4
+ALU = mybir.AluOpType
+ACT = mybir.ActivationFunctionType
+AX = mybir.AxisListType
+
+
+def tile_attgcn_pa_v_kernel(
+    tc, x, A, lam, phi_w, phi_b, theta_w, theta_b, kappa_w, kappa_b, p, th, grad_out, out_0, out_1
+):
+    nc = tc.nc
+    with ExitStack() as ctx:
+        keep = ctx.enter_context(tc.tile_pool(name="keep", bufs=1))
+        gin = ctx.enter_context(tc.tile_pool(name="gin", bufs=3))
+        mid = ctx.enter_context(tc.tile_pool(name="mid", bufs=3))
+        deep = ctx.enter_context(tc.tile_pool(name="deep", bufs=4))
+        two = ctx.enter_context(tc.tile_pool(name="two", bufs=2))
+        work_pool = ctx.enter_context(tc.psum_pool(name="work_pool", bufs=5))
+        part_pool = ctx.enter_context(tc.psum_pool(name="part_pool", bufs=2))
+        dt_pool = ctx.enter_context(tc.psum_pool(name="dt_pool", bufs=1))
+        ctx.enter_context(tc.manual_schedule())
+
+        lam_bf = keep.tile([P, 1], BF16, name="lam_bf")
+        lam_f = keep.tile([P, 1], F32, name="lam_f")
+        ident = keep.tile([P, P], F32, name="ident")
+        fold = keep.tile([P, V], F32, name="fold")
+        warm = keep.tile([P, 1], F32, name="warm")
+        raw_rows = {}
+        p_t = keep.tile([P, PACK, B * V], F32, name="p_t")
+        th_t = keep.tile([P, PACK, B * V], F32, name="th_t")
+        dp_t = keep.tile([P, PACK, B * V], F32, name="dp_t")
+        kap_sb = keep.tile([P, PACK, K], BF16, name="kap_sb", align_bytes=64)
+        kap_q = keep.tile([P, K], U32, name="kap_q", align_bytes=64)
+        kap_s = keep.tile([P, K], U8, name="kap_s", align_bytes=64)
+        w_sb = keep.tile([P, 2, 4, K], BF16, name="w_sb", align_bytes=64)
+        w_q = keep.tile([P, 2, C], U32, name="w_q", align_bytes=64)
+        w_s = keep.tile([P, 2, C], U8, name="w_s", align_bytes=64)
+        x_sb = keep.tile([P, T, PACK * C], BF16, name="x_sb", align_bytes=64)
+        x_q = keep.tile([P, T, C], U32, name="x_q", align_bytes=64)
+        x_s = keep.tile([P, T, C], U8, name="x_s", align_bytes=64)
+        dpm = keep.tile([P, K, PACK], BF16, name="dpm", align_bytes=64)
+        dpm_q = keep.tile([P, K], U32, name="dpm_q", align_bytes=64)
+        dpm_s = keep.tile([P, K], U8, name="dpm_s", align_bytes=64)
+
+        p_rows = p.rearrange("b u c -> (b u) c")
+        th_rows = th.rearrange("b v c -> (b v) c")
+        kap_rows = kappa_w.rearrange("(m t) k -> m t k", t=PACK)
+        g_tiles, il_tiles, q_tiles, s_tiles = {}, {}, {}, {}
+        f_tiles, f2_tiles, df_tiles, ns_tiles = {}, {}, {}, {}
+        part_tiles, parts_sb, dt_tiles = {}, {}, {}
+        banks = {}
+
+        def load_rows(r):
+            rows = slice(r * P, (r + 1) * P)
+            for key, src in (("p", p_rows), ("th", th_rows)):
+                raw = two.tile([P, K], F32, name="raw_" + key)
+                raw_rows[key, r] = raw
+                nc.sync.dma_start(out=raw[:], in_=src[rows, :])
+
+        def load_grad(b):
+            g = gin.tile([P, PACK, TOK], BF16, name="g", align_bytes=64)
+            g_tiles[b] = g
+            src = grad_out[b].rearrange("(p j) u v -> p j (u v)", j=PACK)
+            if b == 0:
+                for h in range(2):
+                    cols = slice(h * HALF, (h + 1) * HALF)
+                    nc.sync.dma_start(out=g[:, :, cols], in_=src[:, :, cols])
+            else:
+                nc.sync.dma_start(out=g[:], in_=src)
+
+        def turn_rows(key):
+            bank = work_pool.tile([P, HALF], F32, name="bank", tag="work")
+            banks[key] = bank
+            for t in range(PACK):
+                nc.tensor.transpose(bank[:, t * P : (t + 1) * P], raw_rows[key][:, t:K:PACK], ident[:])
+
+        def take_rows(dst, key, on_scalar):
+            r = key[1]
+            src = banks[key][:].rearrange("p (t q) -> p t q", t=PACK)
+            out = dst[:, :, r * P : (r + 1) * P]
+            if on_scalar:
+                nc.scalar.copy(out=out, in_=src)
+            else:
+                nc.vector.tensor_copy(out=out, in_=src)
+
+        def turn_words(sb, pair, key):
+            bank = work_pool.tile([P, HALF], F32, name="bank", tag="work")
+            banks[key] = bank
+            for i in range(2):
+                words = sb[:, 2 * pair + i, :].bitcast(F32)
+                for u in range(2):
+                    at = (2 * i + u) * P
+                    nc.tensor.transpose(bank[:, at : at + P], words[:, u : K // 2 : 2], ident[:])
+
+        def take_words(grouped, pair, key, on_scalar):
+            src = banks[key][:].rearrange("p (i u m) -> p i m u", i=2, u=2)
+            flat = grouped[:].rearrange("p c t -> p (c t)").bitcast(F32)
+            out = flat[:, pair * 512 : (pair + 1) * 512].rearrange("p (i m u) -> p i m u", i=2, u=2)
+            if on_scalar:
+                nc.scalar.copy(out=out, in_=src)
+            else:
+                nc.vector.tensor_copy(out=out, in_=src)
+
+        def quantize(codes, scales, grouped, fmt):
+            nc.vector.quantize_mx(
+                out=codes.bitcast(fmt), scales=scales, in_=grouped[:].rearrange("p c t -> p (c t)")
+            )
+
+        def interleave(b, h, engine):
+            il = deep.tile([P, HALF, PACK], BF16, name="il", align_bytes=64)
+            il_tiles[b, h] = il
+            src = g_tiles[b][:, :, h * HALF : (h + 1) * HALF].rearrange("p j n -> p n j")
+            engine.tensor_scalar(
+                out=il[:], in0=src, scalar1=lam_f[:, 0:1], scalar2=0.0, op0=ALU.mult, op1=ALU.add
+            )
+
+        def quant_dz2(b, h):
+            if h == 0:
+                q_tiles[b] = mid.tile([P, TOK], U32, name="dz2_q", align_bytes=64)
+                s_tiles[b] = mid.tile([P, TOK], U8, name="dz2_s", align_bytes=64)
+            cols = slice(h * HALF, (h + 1) * HALF)
+            quantize(q_tiles[b][:, cols], s_tiles[b][:, cols], il_tiles[b, h], E5)
+
+        def tanh(n):
+            b, ct = divmod(n, PACK)
+            f = mid.tile([P, TOK], F32, name="f")
+            f_tiles[n] = f
+            for u in range(V):
+                col = b * V + u
+                nc.scalar.activation(
+                    out=f[:, u * V : (u + 1) * V],
+                    in_=th_t[:, ct, b * V : (b + 1) * V],
+                    func=ACT.Tanh,
+                    bias=p_t[:, ct, col : col + 1],
+                    scale=-1.0,
+                )
+
+        def square(n):
+            f2 = deep.tile([P, TOK], F32, name="f2")
+            f2_tiles[n] = f2
+            f = f_tiles[n]
+            if n % 2 == 1:
+                nc.gpsimd.tensor_tensor(out=f2[:], in0=f[:], in1=f[:], op=ALU.mult)
+            else:
+                nc.scalar.activation(out=f2[:], in_=f[:], func=ACT.Square)
+
+        def multiply(n):
+            b, ct = divmod(n, PACK)
+            w_cols = slice(ct * P, (ct + 1) * P)
+            for h in range(2):
+                cols = slice(h * HALF, (h + 1) * HALF)
+                df = work_pool.tile([P, HALF], F32, name="df", tag="work")
+                df_tiles[n, h] = df
+                nc.tensor.matmul_mx(
+                    out=df[:],
+                    lhsT=kap_q[:, w_cols].bitcast(E4),
+                    lhsT_scale=kap_s[:, w_cols],
+                    rhs=q_tiles[b][:, cols].bitcast(E5),
+                    rhs_scale=s_tiles[b][:, cols],
+                    start=True,
+                    stop=True,
+                )
+
+        def weigh(n):
+            ns = deep.tile([P, TOK], F32, name="ns")
+            ns_tiles[n] = ns
+            for h in range(2):
+                cols = slice(h * HALF, (h + 1) * HALF)
+                nc.vector.scalar_tensor_tensor(
+                    out=ns[:, cols], in0=f2_tiles[n][:, cols], scalar=1.0, in1=df_tiles[n, h][:],
+                    op0=ALU.subtract, op1=ALU.mult,
+                )
+
+        def sum_v(n):
+            b, ct = divmod(n, PACK)
+            nc.vector.tensor_reduce(
+                out=dp_t[:, ct, b * V : (b + 1) * V],
+                in_=ns_tiles[n][:].rearrange("p (u v) -> p u v", v=V),
+                axis=AX.X,
+                op=ALU.add,
+            )
+
+        def sum_u(n):
+            b, ct = divmod(n, PACK)
+            if ct == 0:
+                part_tiles[b] = part_pool.tile([P, HALF], F32, name="part")
+            n_blocks = TOK // P
+            for i in range(n_blocks):
+                nc.tensor.matmul(
+                    part_tiles[b][:, ct * P : (ct + 1) * P],
+                    ns_tiles[n][:, i * P : (i + 1) * P],
+                    ident[:],
+                    start=(i == 0),
+                    stop=(i == n_blocks - 1),
+                    is_transpose=True,
+                )
+
+        def take_part(b):
+            part = two.tile([P, HALF], F32, name="part_sb")
+            parts_sb[b] = part
+            nc.scalar.copy(out=part[:], in_=part_tiles[b][:])
+
+        def fold_part(b):
+            g, i = divmod(b, 4)
+            if i == 0:
+                dt_tiles[g] = dt_pool.tile([P, HALF], F32, name="dt")
+            for ct in range(PACK):
+                at = ct * P + i * V
+                nc.tensor.matmul(
+                    dt_tiles[g][:, at : at + V], parts_sb[b][:, ct * P : (ct + 1) * P], fold[:],
+                    start=True, stop=True,
+                )
+
+        dz1 = {}
+
+        def round_dt(g):
+            grouped = two.tile([P, P, PACK], BF16, name="dt_g", align_bytes=64)
+            dz1[g, 1] = grouped
+            nc.scalar.activation(
+                out=grouped[:], in_=dt_tiles[g][:].rearrange("p (t n) -> p n t", t=PACK), func=ACT.Copy, scale=0.25
+            )
+
+        def round_dp(g):
+            grouped = two.tile([P, P, PACK], BF16, name="dp_g", align_bytes=64)
+            dz1[g, 0] = grouped
+            nc.vector.tensor_scalar(
+                out=grouped[:], in0=dp_t[:, :, g * P : (g + 1) * P].rearrange("p t n -> p n t"),
+                scalar1=-0.25, scalar2=None, op0=ALU.mult,
+            )
+
+        dz1_q = {}
+
+        def quant_dz1(g, i):
+            codes = two.tile([P, P], U32, name="dz1_q%d" % i, align_bytes=64)
+            scales = two.tile([P, P], U8, name="dz1_s%d" % i, align_bytes=64)
+            dz1_q[g, i] = (codes, scales)
+            quantize(codes[:], scales[:], dz1[g, i], E5)
+
+        def product_0(g):
+            bank = work_pool.tile([P, HALF], F32, name="bank", tag="work")
+            banks["o0", g] = bank
+            for i in range(2):
+                codes, scales = dz1_q[g, i]
+                nc.tensor.matmul_mx(
+                    out=bank[:], lhsT=codes[:].bitcast(E5), lhsT_scale=scales[:],
+                    rhs=w_q[:, i, :].bitcast(E4), rhs_scale=w_s[:, i, :],
+                    start=(i == 0), stop=(i == 1),
+                )
+
+        def store_0(g):
+            rows = two.tile([P, C], F32, name="rows")
+            nc.scalar.copy(out=rows[:], in_=banks["o0", g][:])
+            for i in range(4):
+                src = rows[i * V : (i + 1) * V, :].unsqueeze(1).to_broadcast([V, T, C])
+                nc.sync.dma_start(out=out_0[4 * g + i].rearrange("t j c -> j t c"), in_=src)
+
+        x_il = {}
+
+        def interleave_x(t):
+            il = two.tile([P, C, PACK], BF16, name="x_il", align_bytes=64)
+            x_il[t] = il
+            nc.vector.tensor_copy(out=il[:], in_=x_sb[:, t, :].rearrange("p (j c) -> p c j", j=PACK))
+
+        def turn_dp(ct):
+            bank = work_pool.tile([P, HALF], F32, name="bank", tag="work")
+            banks["dp", ct] = bank
+            for t in range(PACK):
+                nc.tensor.transpose(bank[:, t * P : (t + 1) * P], dp_t[:, ct, t : B * V : PACK], ident[:])
+
+        def round_dpm(ct):
+            nc.scalar.activation(
+                out=dpm[:, ct * P : (ct + 1) * P, :],
+                in_=banks["dp", ct][:].rearrange("p (t m) -> p m t", t=PACK), func=ACT.Copy, scale=-0.25,
+            )
+
+        def product_1(m):
+            bank = work_pool.tile([P, HALF], F32, name="bank", tag="work")
+            rows = slice(m * P, (m + 1) * P)
+            for t in range(T):
+                nc.tensor.matmul_mx(
+                    out=bank[:], lhsT=x_q[:, t, rows].bitcast(E4), lhsT_scale=x_s[:, t, rows],
+                    rhs=dpm_q[:].bitcast(E5), rhs_scale=dpm_s[:], start=(t == 0), stop=(t == T - 1),
+                )
+            o = deep.tile([P, K], F32, name="o1")
+            src = bank[:].rearrange("p (t m) -> p m t", t=PACK)
+            dst = o[:].rearrange("p (m t) -> p m t", t=PACK)
+            if m % 2 == 0:
+                nc.vector.tensor_copy(out=dst, in_=src)
+            else:
+                nc.scalar.copy(out=dst, in_=src)
+            nc.sync.dma_start(out=out_1[rows, :], in_=o[:])
+
+        nc.scalar.dma_start(out=lam_bf[:], in_=lam.partition_broadcast(P))
+        load_rows(0)
+        load_grad(0)
+        nc.sync.dma_start(out=kap_sb[:], in_=kap_rows)
+        load_grad(1)
+        make_identity(nc, ident[:])
+        nc.vector.memset(warm[:], 0.0)
+        nc.scalar.activation(out=warm[:], in_=warm[:], func=ACT.Tanh)
+        nc.vector.tensor_copy(out=lam_f[:], in_=lam_bf[:])
+        nc.vector.tensor_reduce(
+            out=fold[:], in_=ident[:].rearrange("p (a v) -> p v a", v=V), axis=AX.X, op=ALU.add
+        )
+        turn_rows(("p", 0))
+        turn_rows(("th", 0))
+        take_rows(p_t, ("p", 0), False)
+        take_rows(th_t, ("th", 0), True)
+        kap_g = keep.tile([P, K, PACK], BF16, name="kap_g", align_bytes=64)
+        turn_words(kap_sb, 0, "k0")
+        turn_words(kap_sb, 1, "k1")
+        interleave(0, 0, nc.vector)
+        interleave(0, 1, nc.gpsimd)
+        tanh(0)
+        take_words(kap_g, 0, "k0", False)
+        take_words(kap_g, 1, "k1", False)
+        quant_dz2(0, 0)
+        quantize(kap_q[:], kap_s[:], kap_g, E4)
+        square(0)
+        tanh(1)
+        square(1)
+        tanh(2)
+        interleave(1, 0, nc.gpsimd)
+        quant_dz2(0, 1)
+        multiply(0)
+
+        side = {}
+
+        def at(step, fn, *args):
+            side.setdefault(step, []).append((fn, args))
+
+        for r in range(1, 4):
+            first = 4 * (4 * r - 3) + 2
+            at(first - 6, load_rows, r)
+            at(first, turn_rows, ("p", r))
+            at(first + 1, take_rows, p_t, ("p", r), True)
+            at(first + 2, turn_rows, ("th", r))
+            at(first + 3, take_rows, th_t, ("th", r), False)
+        w_g = {}
+
+        def load_weights():
+            for i, w in enumerate((phi_w, theta_w)):
+                nc.sync.dma_start(out=w_sb[:, i, :, :], in_=w.rearrange("(r m) k -> m r k", m=P))
+
+        def new_w(i):
+            w_g[i] = two.tile([P, C, PACK], BF16, name="w_g", align_bytes=64)
+
+        def take_w(i, pair, on_scalar):
+            take_words(w_g[i], pair, ("w", i, pair), on_scalar)
+
+        def quant_w(i):
+            quantize(w_q[:, i, :], w_s[:, i, :], w_g[i], E4)
+
+        at(2, load_weights)
+        for i in range(2):
+            first = 10 + 4 * i
+            at(first, new_w, i)
+            for pair in range(2):
+                at(first + 2 * pair, turn_words, w_sb[:, i, :, :], pair, ("w", i, pair))
+                at(first + 2 * pair + 1, take_w, i, pair, pair == 0)
+            at(first + 5, quant_w, i)
+
+        def load_x(q):
+            src = x[:, :, q * PACK : (q + 1) * PACK, :].rearrange("b t j c -> b t (j c)")
+            nc.sync.dma_start(out=x_sb[q : P : 8, :, :], in_=src)
+
+        for q in range(8):
+            at(13 + q, load_x, q)
+
+        def quant_x(t):
+            quantize(x_q[:, t, :], x_s[:, t, :], x_il[t], E4)
+
+        for t in range(T):
+            at(31 + 7 * t, interleave_x, t)
+            at(33 + 7 * t, quant_x, t)
+
+        for b in range(B):
+            if b + 2 < B:
+                at(4 * b - 1, load_grad, b + 2)
+            if b + 1 < B:
+                if b > 0:
+                    at(4 * b - 2, interleave, b + 1, 0, nc.gpsimd)
+                at(4 * b, interleave, b + 1, 1, nc.gpsimd)
+                at(4 * b + 1, quant_dz2, b + 1, 0)
+                at(4 * b + 2, quant_dz2, b + 1, 1)
+            at(4 * b + 5, take_part, b)
+            at(4 * b + 6, fold_part, b)
+            if b % 4 == 3:
+                g = b // 4
+                at(4 * b + 5, round_dp, g)
+                at(4 * b + 7, round_dt, g)
+                at(4 * b + 7, quant_dz1, g, 0)
+                at(4 * b + 8, quant_dz1, g, 1)
+                at(4 * b + 8, product_0, g)
+                at(4 * b + 9, store_0, g)
+        for ct in range(PACK):
+            at(N_UNITS - 3 + ct, turn_dp, ct)
+            at(N_UNITS - 2 + ct, round_dpm, ct)
+
+        def quant_dpm():
+            quantize(dpm_q[:], dpm_s[:], dpm, E5)
+
+        at(N_UNITS + 2, quant_dpm)
+        for m in range(4):
+            at(N_UNITS + 3 + m, product_1, m)
+
+        for s in range(-1, N_UNITS + 10):
+            if 3 <= s + 3 < N_UNITS:
+                tanh(s + 3)
+            if 2 <= s + 2 < N_UNITS:
+                square(s + 2)
+            if 1 <= s + 1 < N_UNITS:
+                multiply(s + 1)
+            if 0 <= s < N_UNITS:
+                weigh(s)
+            if 0 <= s - 1 < N_UNITS:
+                sum_v(s - 1)
+                sum_u(s - 1)
+            for fn, args in side.get(s, []):
+                fn(*args)

@@ -9,6 +9,22 @@ PACK = 4
 TOK = V * V
 HALF = 512
 N_UNITS = B * PACK
+LEAD = 4
+F_BUFS = 4
+Q_STEP = 1
+PE_CT = (1,)
+IL_BUFS = 1
+PIECES = (256, 256, 512)
+GP_COLS = 0
+DUP = 0
+WORK = 5
+PV_LAG = 3
+PART_LAG = 5
+ROWS_LAG = 1
+ROWS_ON_V = True
+PV_N = 128
+V_HEAD = 3
+PART_ON_V = False
 FLOPS = 2 * B * TOK * K * K + 2 * (B * V) * (2 * K) * C + 2 * T * C * (B * V) * K
 BYTES = (
     B * T * V * C * 2 + 3 * C * K * 2 + 2 * B * V * K * 4 + B * K * TOK * 2 + 2
@@ -36,15 +52,19 @@ def tile_attgcn_pa_v_kernel(
         mid = ctx.enter_context(tc.tile_pool(name="mid", bufs=3))
         deep = ctx.enter_context(tc.tile_pool(name="deep", bufs=4))
         two = ctx.enter_context(tc.tile_pool(name="two", bufs=2))
-        work_pool = ctx.enter_context(tc.psum_pool(name="work_pool", bufs=5))
-        part_pool = ctx.enter_context(tc.psum_pool(name="part_pool", bufs=2))
+        work_pool = ctx.enter_context(tc.psum_pool(name="work_pool", bufs=WORK))
+        part_pool = ctx.enter_context(tc.psum_pool(name="part_pool", bufs=6 - WORK))
+        pv_pool = ctx.enter_context(tc.psum_pool(name="pv_pool", bufs=1))
         dt_pool = ctx.enter_context(tc.psum_pool(name="dt_pool", bufs=1))
+        il_pool = ctx.enter_context(tc.tile_pool(name="il_pool", bufs=IL_BUFS))
+        f_pool = ctx.enter_context(tc.tile_pool(name="f_pool", bufs=F_BUFS))
         ctx.enter_context(tc.manual_schedule())
 
         lam_bf = keep.tile([P, 1], BF16, name="lam_bf")
         lam_f = keep.tile([P, 1], F32, name="lam_f")
         ident = keep.tile([P, P], F32, name="ident")
-        fold = keep.tile([P, V], F32, name="fold")
+        fold = keep.tile([P, P], F32, name="fold")
+        fold_v = keep.tile([P, P], F32, name="fold_v")
         warm = keep.tile([P, 1], F32, name="warm")
         raw_rows = {}
         p_t = keep.tile([P, PACK, B * V], F32, name="p_t")
@@ -128,23 +148,24 @@ def tile_attgcn_pa_v_kernel(
             )
 
         def interleave(b, h, engine):
-            il = deep.tile([P, HALF, PACK], BF16, name="il", align_bytes=64)
-            il_tiles[b, h] = il
-            src = g_tiles[b][:, :, h * HALF : (h + 1) * HALF].rearrange("p j n -> p n j")
+            if h == 0:
+                il_tiles[b] = il_pool.tile([P, TOK, PACK], BF16, name="il", align_bytes=64)
+            cols = slice(h * HALF, (h + 1) * HALF)
             engine.tensor_scalar(
-                out=il[:], in0=src, scalar1=lam_f[:, 0:1], scalar2=0.0, op0=ALU.mult, op1=ALU.add
+                out=il_tiles[b][:, cols, :], in0=g_tiles[b][:, :, cols].rearrange("p j n -> p n j"),
+                scalar1=lam_f[:, 0:1], scalar2=0.0, op0=ALU.mult, op1=ALU.add,
             )
 
-        def quant_dz2(b, h):
-            if h == 0:
+        def quant_dz2(b, lo, hi):
+            if lo == 0:
                 q_tiles[b] = mid.tile([P, TOK], U32, name="dz2_q", align_bytes=64)
                 s_tiles[b] = mid.tile([P, TOK], U8, name="dz2_s", align_bytes=64)
-            cols = slice(h * HALF, (h + 1) * HALF)
-            quantize(q_tiles[b][:, cols], s_tiles[b][:, cols], il_tiles[b, h], E5)
+            cols = slice(lo, hi)
+            quantize(q_tiles[b][:, cols], s_tiles[b][:, cols], il_tiles[b][:, cols, :], E5)
 
         def tanh(n):
             b, ct = divmod(n, PACK)
-            f = mid.tile([P, TOK], F32, name="f")
+            f = f_pool.tile([P, TOK], F32, name="f")
             f_tiles[n] = f
             for u in range(V):
                 col = b * V + u
@@ -156,14 +177,29 @@ def tile_attgcn_pa_v_kernel(
                     scale=-1.0,
                 )
 
-        def square(n):
-            f2 = deep.tile([P, TOK], F32, name="f2")
-            f2_tiles[n] = f2
-            f = f_tiles[n]
-            if n % 2 == 1:
-                nc.gpsimd.tensor_tensor(out=f2[:], in0=f[:], in1=f[:], op=ALU.mult)
+        def square_cols(n, lo, hi, on_scalar):
+            if n not in f2_tiles:
+                f2_tiles[n] = deep.tile([P, TOK], F32, name="f2")
+            f2, f = f2_tiles[n], f_tiles[n]
+            if on_scalar:
+                nc.scalar.activation(out=f2[:, lo:hi], in_=f[:, lo:hi], func=ACT.Square)
             else:
-                nc.scalar.activation(out=f2[:], in_=f[:], func=ACT.Square)
+                nc.gpsimd.tensor_tensor(out=f2[:, lo:hi], in0=f[:, lo:hi], in1=f[:, lo:hi], op=ALU.mult)
+
+        def gp_share(n):
+            if n < 7:
+                return 0
+            if n >= 61 or n % 4 == 3:
+                return sum(PIECES)
+            return GP_COLS if n % 4 == 2 else 0
+
+        def square(n):
+            g = gp_share(n)
+            if n < V_HEAD:
+                f2_tiles[n] = deep.tile([P, TOK], F32, name="f2")
+                nc.vector.tensor_tensor(out=f2_tiles[n][:], in0=f_tiles[n][:], in1=f_tiles[n][:], op=ALU.mult)
+            elif g < TOK:
+                square_cols(n, g, TOK, True)
 
         def multiply(n):
             b, ct = divmod(n, PACK)
@@ -172,15 +208,16 @@ def tile_attgcn_pa_v_kernel(
                 cols = slice(h * HALF, (h + 1) * HALF)
                 df = work_pool.tile([P, HALF], F32, name="df", tag="work")
                 df_tiles[n, h] = df
-                nc.tensor.matmul_mx(
-                    out=df[:],
-                    lhsT=kap_q[:, w_cols].bitcast(E4),
-                    lhsT_scale=kap_s[:, w_cols],
-                    rhs=q_tiles[b][:, cols].bitcast(E5),
-                    rhs_scale=s_tiles[b][:, cols],
-                    start=True,
-                    stop=True,
-                )
+                for i in range(1 + (DUP if h == 0 else 0)):
+                    nc.tensor.matmul_mx(
+                        out=df[:],
+                        lhsT=kap_q[:, w_cols].bitcast(E4),
+                        lhsT_scale=kap_s[:, w_cols],
+                        rhs=q_tiles[b][:, cols].bitcast(E5),
+                        rhs_scale=s_tiles[b][:, cols],
+                        start=True,
+                        stop=True,
+                    )
 
         def weigh(n):
             ns = deep.tile([P, TOK], F32, name="ns")
@@ -216,30 +253,55 @@ def tile_attgcn_pa_v_kernel(
                     is_transpose=True,
                 )
 
-        def take_part(b):
+        def on_tensor(n):
+            return n % PACK in PE_CT and n < N_UNITS - PACK
+
+        pv, pv_sb = {}, {}
+
+        def sum_v_tensor(n):
+            pv[n] = pv_pool.tile([P, P + PV_N], F32, name="pv")
+            for r in range(8):
+                nc.tensor.matmul(
+                    pv[n][:, 0:P], ns_tiles[n][:, r:TOK:8], ident[:], start=(r == 0), stop=(r == 7), is_transpose=True
+                )
+
+        def take_pv(n):
+            pv_sb[n] = two.tile([P, P], F32, name="pv_sb")
+            nc.vector.tensor_copy(out=pv_sb[n][:], in_=pv[n][:, 0:P])
+
+        def fold_pv(n):
+            nc.tensor.matmul(pv[n][:, P : P + PV_N], pv_sb[n][:], fold_v[:, 0:PV_N], start=True, stop=True)
+
+        def keep_pv(n):
+            b, ct = divmod(n, PACK)
+            nc.vector.tensor_copy(out=dp_t[:, ct, b * V : (b + 1) * V], in_=pv[n][:, P : P + V])
+
+        def take_part(b, on_vector):
             part = two.tile([P, HALF], F32, name="part_sb")
             parts_sb[b] = part
-            nc.scalar.copy(out=part[:], in_=part_tiles[b][:])
+            if on_vector:
+                nc.vector.tensor_copy(out=part[:], in_=part_tiles[b][:])
+            else:
+                nc.scalar.copy(out=part[:], in_=part_tiles[b][:])
 
-        def fold_part(b):
-            g, i = divmod(b, 4)
-            if i == 0:
-                dt_tiles[g] = dt_pool.tile([P, HALF], F32, name="dt")
-            for ct in range(PACK):
-                at = ct * P + i * V
-                nc.tensor.matmul(
-                    dt_tiles[g][:, at : at + V], parts_sb[b][:, ct * P : (ct + 1) * P], fold[:],
-                    start=True, stop=True,
-                )
+        def fold_part(b, ct):
+            if ct == 0:
+                dt_tiles[b] = dt_pool.tile([P, HALF], F32, name="dt")
+            cols = slice(ct * P, (ct + 1) * P)
+            nc.tensor.matmul(dt_tiles[b][:, cols], parts_sb[b][:, cols], fold[:], start=True, stop=True)
 
         dz1 = {}
 
-        def round_dt(g):
-            grouped = two.tile([P, P, PACK], BF16, name="dt_g", align_bytes=64)
-            dz1[g, 1] = grouped
-            nc.scalar.activation(
-                out=grouped[:], in_=dt_tiles[g][:].rearrange("p (t n) -> p n t", t=PACK), func=ACT.Copy, scale=0.25
-            )
+        def round_dt(b):
+            g, i = divmod(b, 4)
+            if i == 0:
+                dz1[g, 1] = two.tile([P, P, PACK], BF16, name="dt_g", align_bytes=64)
+            src = dt_tiles[b][:].rearrange("p (t a v) -> p a v t", t=PACK, v=V)[:, 0, :, :]
+            out = dz1[g, 1][:, i * V : (i + 1) * V, :]
+            if ROWS_ON_V and b < 15:
+                nc.vector.tensor_scalar(out=out, in0=src, scalar1=0.25, scalar2=None, op0=ALU.mult)
+            else:
+                nc.scalar.activation(out=out, in_=src, func=ACT.Copy, scale=0.25)
 
         def round_dp(g):
             grouped = two.tile([P, P, PACK], BF16, name="dp_g", align_bytes=64)
@@ -270,7 +332,10 @@ def tile_attgcn_pa_v_kernel(
 
         def store_0(g):
             rows = two.tile([P, C], F32, name="rows")
-            nc.scalar.copy(out=rows[:], in_=banks["o0", g][:])
+            if ROWS_ON_V and g < 3:
+                nc.vector.tensor_copy(out=rows[:], in_=banks["o0", g][:])
+            else:
+                nc.scalar.copy(out=rows[:], in_=banks["o0", g][:])
             for i in range(4):
                 src = rows[i * V : (i + 1) * V, :].unsqueeze(1).to_broadcast([V, T, C])
                 nc.sync.dma_start(out=out_0[4 * g + i].rearrange("t j c -> j t c"), in_=src)
@@ -320,9 +385,14 @@ def tile_attgcn_pa_v_kernel(
         nc.vector.memset(warm[:], 0.0)
         nc.scalar.activation(out=warm[:], in_=warm[:], func=ACT.Tanh)
         nc.vector.tensor_copy(out=lam_f[:], in_=lam_bf[:])
-        nc.vector.tensor_reduce(
-            out=fold[:], in_=ident[:].rearrange("p (a v) -> p v a", v=V), axis=AX.X, op=ALU.add
-        )
+        for a in range(4):
+            nc.vector.tensor_reduce(
+                out=fold[:, a * V : (a + 1) * V], in_=ident[:].rearrange("p (a v) -> p v a", v=V), axis=AX.X, op=ALU.add
+            )
+        for a in range(PV_N // V):
+            nc.vector.tensor_reduce(
+                out=fold_v[:, a * V : (a + 1) * V], in_=ident[:].rearrange("p (v a) -> p v a", v=V), axis=AX.X, op=ALU.add
+            )
         turn_rows(("p", 0))
         turn_rows(("th", 0))
         take_rows(p_t, ("p", 0), False)
@@ -335,14 +405,16 @@ def tile_attgcn_pa_v_kernel(
         tanh(0)
         take_words(kap_g, 0, "k0", False)
         take_words(kap_g, 1, "k1", False)
-        quant_dz2(0, 0)
+        quant_dz2(0, 0, HALF)
         quantize(kap_q[:], kap_s[:], kap_g, E4)
         square(0)
         tanh(1)
         square(1)
         tanh(2)
+        tanh(3)
+        quant_dz2(0, HALF, TOK)
         interleave(1, 0, nc.gpsimd)
-        quant_dz2(0, 1)
+        interleave(1, 1, nc.gpsimd)
         multiply(0)
 
         side = {}
@@ -351,10 +423,10 @@ def tile_attgcn_pa_v_kernel(
             side.setdefault(step, []).append((fn, args))
 
         for r in range(1, 4):
-            first = 4 * (4 * r - 3) + 2
-            at(first - 6, load_rows, r)
+            first = 4 * (4 * r - 3)
+            at(first - 5, load_rows, r)
             at(first, turn_rows, ("p", r))
-            at(first + 1, take_rows, p_t, ("p", r), True)
+            at(first + 1, take_rows, p_t, ("p", r), not ROWS_ON_V)
             at(first + 2, turn_rows, ("th", r))
             at(first + 3, take_rows, th_t, ("th", r), False)
         w_g = {}
@@ -374,11 +446,11 @@ def tile_attgcn_pa_v_kernel(
 
         at(2, load_weights)
         for i in range(2):
-            first = 10 + 4 * i
+            first = 8 + 4 * i
             at(first, new_w, i)
             for pair in range(2):
                 at(first + 2 * pair, turn_words, w_sb[:, i, :, :], pair, ("w", i, pair))
-                at(first + 2 * pair + 1, take_w, i, pair, pair == 0)
+                at(first + 2 * pair + 1, take_w, i, pair, pair == 0 and not ROWS_ON_V)
             at(first + 5, quant_w, i)
 
         def load_x(q):
@@ -392,28 +464,46 @@ def tile_attgcn_pa_v_kernel(
             quantize(x_q[:, t, :], x_s[:, t, :], x_il[t], E4)
 
         for t in range(T):
-            at(31 + 7 * t, interleave_x, t)
-            at(33 + 7 * t, quant_x, t)
+            at(4 * (6 + t) + Q_STEP, interleave_x, t)
+            at(4 * (7 + t) + Q_STEP, quant_x, t)
 
+        for b in range(B):
+            last = b == B - 1
+            if b % 4 == 3:
+                g = b // 4
+                at(4 * b + 7, round_dp, g)
+                at(4 * b + (8 if last else 4 + Q_STEP + 4), quant_dz1, g, 0)
+                at(4 * b + (8 if last else 12 + Q_STEP), quant_dz1, g, 1)
+                at(4 * b + (8 if last else 12 + Q_STEP), product_0, g)
+                at(4 * b + (9 if last else 13 + Q_STEP), store_0, g)
         for b in range(B):
             if b + 2 < B:
                 at(4 * b - 1, load_grad, b + 2)
             if b + 1 < B:
-                if b > 0:
-                    at(4 * b - 2, interleave, b + 1, 0, nc.gpsimd)
-                at(4 * b, interleave, b + 1, 1, nc.gpsimd)
-                at(4 * b + 1, quant_dz2, b + 1, 0)
-                at(4 * b + 2, quant_dz2, b + 1, 1)
-            at(4 * b + 5, take_part, b)
-            at(4 * b + 6, fold_part, b)
-            if b % 4 == 3:
-                g = b // 4
-                at(4 * b + 5, round_dp, g)
-                at(4 * b + 7, round_dt, g)
-                at(4 * b + 7, quant_dz1, g, 0)
-                at(4 * b + 8, quant_dz1, g, 1)
-                at(4 * b + 8, product_0, g)
-                at(4 * b + 9, store_0, g)
+                at(4 * b + Q_STEP, quant_dz2, b + 1, 0, TOK)
+            if b + 2 < B:
+                at(4 * b + Q_STEP + 1, interleave, b + 2, 0, nc.gpsimd)
+            n = 4 * b + 6
+            if 7 <= n < N_UNITS and gp_share(n):
+                at(4 * b + 3, square_cols, n, 0, gp_share(n), False)
+            if b + 2 < B:
+                at(4 * b + Q_STEP + 1, interleave, b + 2, 1, nc.gpsimd)
+            for n in (4 * b + 7,) if b < 14 else (61, 62, 63) if b == 14 else ():
+                lo = 0
+                for w in PIECES:
+                    at(n - 3, square_cols, n, lo, lo + w, False)
+                    lo += w
+            last = b == B - 1
+            at(4 * b + (5 if last else PART_LAG), take_part, b, PART_ON_V and not last)
+            for ct in range(PACK):
+                at(4 * b + (6 if last else PART_LAG + 1 + ct), fold_part, b, ct)
+            at(4 * b + (7 if last else PART_LAG + 5), round_dt, b)
+        for n in range(N_UNITS):
+            if on_tensor(n):
+                at(n + 2, sum_v_tensor, n)
+                at(n + PV_LAG, take_pv, n)
+                at(n + PV_LAG + 1, fold_pv, n)
+                at(n + PV_LAG + 2, keep_pv, n)
         for ct in range(PACK):
             at(N_UNITS - 3 + ct, turn_dp, ct)
             at(N_UNITS - 2 + ct, round_dpm, ct)
@@ -425,17 +515,19 @@ def tile_attgcn_pa_v_kernel(
         for m in range(4):
             at(N_UNITS + 3 + m, product_1, m)
 
+
         for s in range(-1, N_UNITS + 10):
-            if 3 <= s + 3 < N_UNITS:
-                tanh(s + 3)
+            if 4 <= s + LEAD < N_UNITS:
+                tanh(s + LEAD)
             if 2 <= s + 2 < N_UNITS:
                 square(s + 2)
             if 1 <= s + 1 < N_UNITS:
                 multiply(s + 1)
             if 0 <= s < N_UNITS:
                 weigh(s)
-            if 0 <= s - 1 < N_UNITS:
+            if 0 <= s - 1 < N_UNITS and not on_tensor(s - 1):
                 sum_v(s - 1)
-                sum_u(s - 1)
+            if 0 <= s - 2 < N_UNITS:
+                sum_u(s - 2)
             for fn, args in side.get(s, []):
                 fn(*args)

@@ -12,19 +12,22 @@ N_UNITS = B * PACK
 LEAD = 4
 F_BUFS = 4
 Q_STEP = 1
-PE_CT = (1,)
-IL_BUFS = 1
+PE_CT = (2,)
+PE_ODD = ()
 PIECES = (256, 256, 512)
 GP_COLS = 0
-DUP = 0
-WORK = 5
-PV_LAG = 3
-PART_LAG = 5
-ROWS_LAG = 1
-ROWS_ON_V = True
-PV_N = 128
+WORK = 4
+TP_BUFS = 2
 V_HEAD = 3
-PART_ON_V = False
+G_HEAD = ()
+SCALAR_TP = (0, 2)
+SCALAR_MISC = False
+LAG_T = 2
+LAG_C = 3
+LAG_R = 4
+LAG_K = 5
+FOLD_N = 128
+LONE_N = 128
 FLOPS = 2 * B * TOK * K * K + 2 * (B * V) * (2 * K) * C + 2 * T * C * (B * V) * K
 BYTES = (
     B * T * V * C * 2 + 3 * C * K * 2 + 2 * B * V * K * 4 + B * K * TOK * 2 + 2
@@ -53,23 +56,23 @@ def tile_attgcn_pa_v_kernel(
         deep = ctx.enter_context(tc.tile_pool(name="deep", bufs=4))
         two = ctx.enter_context(tc.tile_pool(name="two", bufs=2))
         work_pool = ctx.enter_context(tc.psum_pool(name="work_pool", bufs=WORK))
-        part_pool = ctx.enter_context(tc.psum_pool(name="part_pool", bufs=6 - WORK))
-        pv_pool = ctx.enter_context(tc.psum_pool(name="pv_pool", bufs=1))
-        dt_pool = ctx.enter_context(tc.psum_pool(name="dt_pool", bufs=1))
-        il_pool = ctx.enter_context(tc.tile_pool(name="il_pool", bufs=IL_BUFS))
+        tp_pool = ctx.enter_context(tc.psum_pool(name="tp_pool", bufs=TP_BUFS))
+        rr_pool = ctx.enter_context(tc.psum_pool(name="rr_pool", bufs=8 - WORK - TP_BUFS))
+        il_pool = ctx.enter_context(tc.tile_pool(name="il_pool", bufs=1))
         f_pool = ctx.enter_context(tc.tile_pool(name="f_pool", bufs=F_BUFS))
         ctx.enter_context(tc.manual_schedule())
 
         lam_bf = keep.tile([P, 1], BF16, name="lam_bf")
         lam_f = keep.tile([P, 1], F32, name="lam_f")
         ident = keep.tile([P, P], F32, name="ident")
-        fold = keep.tile([P, P], F32, name="fold")
-        fold_v = keep.tile([P, P], F32, name="fold_v")
+        fold_u = keep.tile([P, 2 * P], F32, name="fold_u")
+        fold_v = keep.tile([P, 2 * P], F32, name="fold_v")
         warm = keep.tile([P, 1], F32, name="warm")
         raw_rows = {}
         p_t = keep.tile([P, PACK, B * V], F32, name="p_t")
         th_t = keep.tile([P, PACK, B * V], F32, name="th_t")
-        dp_t = keep.tile([P, PACK, B * V], F32, name="dp_t")
+        d_t = keep.tile([P, 2, PACK, B * V], F32, name="d_t")
+        dp_t = d_t[:, 0, :, :]
         kap_sb = keep.tile([P, PACK, K], BF16, name="kap_sb", align_bytes=64)
         kap_q = keep.tile([P, K], U32, name="kap_q", align_bytes=64)
         kap_s = keep.tile([P, K], U8, name="kap_s", align_bytes=64)
@@ -88,7 +91,7 @@ def tile_attgcn_pa_v_kernel(
         kap_rows = kappa_w.rearrange("(m t) k -> m t k", t=PACK)
         g_tiles, il_tiles, q_tiles, s_tiles = {}, {}, {}, {}
         f_tiles, f2_tiles, df_tiles, ns_tiles = {}, {}, {}, {}
-        part_tiles, parts_sb, dt_tiles = {}, {}, {}
+        tp_tiles, tp_sb, rr_tiles = {}, {}, {}
         banks = {}
 
         def load_rows(r):
@@ -106,6 +109,8 @@ def tile_attgcn_pa_v_kernel(
                 for h in range(2):
                     cols = slice(h * HALF, (h + 1) * HALF)
                     nc.sync.dma_start(out=g[:, :, cols], in_=src[:, :, cols])
+                    if h == 0:
+                        nc.sync.dma_start(out=kap_sb[:], in_=kap_rows)
             else:
                 nc.sync.dma_start(out=g[:], in_=src)
 
@@ -187,6 +192,8 @@ def tile_attgcn_pa_v_kernel(
                 nc.gpsimd.tensor_tensor(out=f2[:, lo:hi], in0=f[:, lo:hi], in1=f[:, lo:hi], op=ALU.mult)
 
         def gp_share(n):
+            if n in G_HEAD:
+                return TOK
             if n < 7:
                 return 0
             if n >= 61 or n % 4 == 3:
@@ -208,16 +215,15 @@ def tile_attgcn_pa_v_kernel(
                 cols = slice(h * HALF, (h + 1) * HALF)
                 df = work_pool.tile([P, HALF], F32, name="df", tag="work")
                 df_tiles[n, h] = df
-                for i in range(1 + (DUP if h == 0 else 0)):
-                    nc.tensor.matmul_mx(
-                        out=df[:],
-                        lhsT=kap_q[:, w_cols].bitcast(E4),
-                        lhsT_scale=kap_s[:, w_cols],
-                        rhs=q_tiles[b][:, cols].bitcast(E5),
-                        rhs_scale=s_tiles[b][:, cols],
-                        start=True,
-                        stop=True,
-                    )
+                nc.tensor.matmul_mx(
+                    out=df[:],
+                    lhsT=kap_q[:, w_cols].bitcast(E4),
+                    lhsT_scale=kap_s[:, w_cols],
+                    rhs=q_tiles[b][:, cols].bitcast(E5),
+                    rhs_scale=s_tiles[b][:, cols],
+                    start=True,
+                    stop=True,
+                )
 
         def weigh(n):
             ns = deep.tile([P, TOK], F32, name="ns")
@@ -238,78 +244,66 @@ def tile_attgcn_pa_v_kernel(
                 op=ALU.add,
             )
 
-        def sum_u(n):
-            b, ct = divmod(n, PACK)
-            if ct == 0:
-                part_tiles[b] = part_pool.tile([P, HALF], F32, name="part")
-            n_blocks = TOK // P
-            for i in range(n_blocks):
-                nc.tensor.matmul(
-                    part_tiles[b][:, ct * P : (ct + 1) * P],
-                    ns_tiles[n][:, i * P : (i + 1) * P],
-                    ident[:],
-                    start=(i == 0),
-                    stop=(i == n_blocks - 1),
-                    is_transpose=True,
-                )
-
         def on_tensor(n):
-            return n % PACK in PE_CT and n < N_UNITS - PACK
+            return (n % PACK in PE_CT or (n % 8 in PE_ODD)) and n < N_UNITS - PACK
 
-        pv, pv_sb = {}, {}
-
-        def sum_v_tensor(n):
-            pv[n] = pv_pool.tile([P, P + PV_N], F32, name="pv")
-            for r in range(8):
+        def turn_sums(n):
+            tp_tiles[n] = tp_pool.tile([P, 2 * P], F32, name="tp")
+            ns = ns_tiles[n]
+            for i in range(8):
                 nc.tensor.matmul(
-                    pv[n][:, 0:P], ns_tiles[n][:, r:TOK:8], ident[:], start=(r == 0), stop=(r == 7), is_transpose=True
+                    tp_tiles[n][:, 0:P], ns[:, i * P : (i + 1) * P], ident[:],
+                    start=(i == 0), stop=(i == 7), is_transpose=True,
+                )
+            if on_tensor(n):
+                for i in range(8):
+                    nc.tensor.matmul(
+                        tp_tiles[n][:, P : 2 * P], ns[:, i:TOK:8], ident[:],
+                        start=(i == 0), stop=(i == 7), is_transpose=True,
+                    )
+
+        def width(n):
+            return 2 if on_tensor(n) else 1
+
+        def take_sums(n):
+            tp_sb[n] = mid.tile([P, 2 * P], F32, name="tp_sb")
+            cols = slice(0, width(n) * P)
+            if n % PACK in SCALAR_TP or n >= 60:
+                nc.scalar.copy(out=tp_sb[n][:, cols], in_=tp_tiles[n][:, cols])
+            else:
+                nc.vector.tensor_copy(out=tp_sb[n][:, cols], in_=tp_tiles[n][:, cols])
+
+        def fold_sums(n):
+            rr_tiles[n] = rr_pool.tile([P, 2 * P], F32, name="rr")
+            for i in range(width(n)):
+                wide = FOLD_N if width(n) == 2 else LONE_N
+                cols = slice(i * P, i * P + wide)
+                nc.tensor.matmul(
+                    rr_tiles[n][:, cols], tp_sb[n][:, i * P : (i + 1) * P], (fold_u, fold_v)[i][:, 0:wide],
+                    start=True, stop=True,
                 )
 
-        def take_pv(n):
-            pv_sb[n] = two.tile([P, P], F32, name="pv_sb")
-            nc.vector.tensor_copy(out=pv_sb[n][:], in_=pv[n][:, 0:P])
-
-        def fold_pv(n):
-            nc.tensor.matmul(pv[n][:, P : P + PV_N], pv_sb[n][:], fold_v[:, 0:PV_N], start=True, stop=True)
-
-        def keep_pv(n):
+        def keep_sums(n):
             b, ct = divmod(n, PACK)
-            nc.vector.tensor_copy(out=dp_t[:, ct, b * V : (b + 1) * V], in_=pv[n][:, P : P + V])
-
-        def take_part(b, on_vector):
-            part = two.tile([P, HALF], F32, name="part_sb")
-            parts_sb[b] = part
-            if on_vector:
-                nc.vector.tensor_copy(out=part[:], in_=part_tiles[b][:])
+            cols = slice(b * V, (b + 1) * V)
+            if on_tensor(n):
+                nc.vector.tensor_copy(out=d_t[:, 0, ct, cols], in_=rr_tiles[n][:, P : P + V])
+            if n >= 60:
+                nc.scalar.copy(out=d_t[:, 1, ct, cols], in_=rr_tiles[n][:, 0:V])
             else:
-                nc.scalar.copy(out=part[:], in_=part_tiles[b][:])
-
-        def fold_part(b, ct):
-            if ct == 0:
-                dt_tiles[b] = dt_pool.tile([P, HALF], F32, name="dt")
-            cols = slice(ct * P, (ct + 1) * P)
-            nc.tensor.matmul(dt_tiles[b][:, cols], parts_sb[b][:, cols], fold[:], start=True, stop=True)
+                nc.vector.tensor_copy(out=d_t[:, 1, ct, cols], in_=rr_tiles[n][:, 0:V])
 
         dz1 = {}
 
-        def round_dt(b):
-            g, i = divmod(b, 4)
-            if i == 0:
-                dz1[g, 1] = two.tile([P, P, PACK], BF16, name="dt_g", align_bytes=64)
-            src = dt_tiles[b][:].rearrange("p (t a v) -> p a v t", t=PACK, v=V)[:, 0, :, :]
-            out = dz1[g, 1][:, i * V : (i + 1) * V, :]
-            if ROWS_ON_V and b < 15:
-                nc.vector.tensor_scalar(out=out, in0=src, scalar1=0.25, scalar2=None, op0=ALU.mult)
+        def round_dz1(g, i):
+            grouped = two.tile([P, P, PACK], BF16, name="dz1_g%d" % i, align_bytes=64)
+            dz1[g, i] = grouped
+            src = d_t[:, i, :, g * P : (g + 1) * P].rearrange("p t n -> p n t")
+            factor = (-0.25, 0.25)[i]
+            if SCALAR_MISC or g == 3:
+                nc.scalar.activation(out=grouped[:], in_=src, func=ACT.Copy, scale=factor)
             else:
-                nc.scalar.activation(out=out, in_=src, func=ACT.Copy, scale=0.25)
-
-        def round_dp(g):
-            grouped = two.tile([P, P, PACK], BF16, name="dp_g", align_bytes=64)
-            dz1[g, 0] = grouped
-            nc.vector.tensor_scalar(
-                out=grouped[:], in0=dp_t[:, :, g * P : (g + 1) * P].rearrange("p t n -> p n t"),
-                scalar1=-0.25, scalar2=None, op0=ALU.mult,
-            )
+                nc.vector.tensor_scalar(out=grouped[:], in0=src, scalar1=factor, scalar2=None, op0=ALU.mult)
 
         dz1_q = {}
 
@@ -332,7 +326,7 @@ def tile_attgcn_pa_v_kernel(
 
         def store_0(g):
             rows = two.tile([P, C], F32, name="rows")
-            if ROWS_ON_V and g < 3:
+            if not SCALAR_MISC and g < 3:
                 nc.vector.tensor_copy(out=rows[:], in_=banks["o0", g][:])
             else:
                 nc.scalar.copy(out=rows[:], in_=banks["o0", g][:])
@@ -342,10 +336,13 @@ def tile_attgcn_pa_v_kernel(
 
         x_il = {}
 
-        def interleave_x(t):
-            il = two.tile([P, C, PACK], BF16, name="x_il", align_bytes=64)
-            x_il[t] = il
-            nc.vector.tensor_copy(out=il[:], in_=x_sb[:, t, :].rearrange("p (j c) -> p c j", j=PACK))
+        def interleave_x(i):
+            t, h = divmod(i, 2)
+            if h == 0:
+                x_il[t] = two.tile([P, C, PACK], BF16, name="x_il", align_bytes=64)
+            cols = slice(h * C // 2, (h + 1) * C // 2)
+            src = x_sb[:, t, :].rearrange("p (j c) -> p c j", j=PACK)[:, cols, :]
+            nc.vector.tensor_copy(out=x_il[t][:, cols, :], in_=src)
 
         def turn_dp(ct):
             bank = work_pool.tile([P, HALF], F32, name="bank", tag="work")
@@ -379,20 +376,16 @@ def tile_attgcn_pa_v_kernel(
         nc.scalar.dma_start(out=lam_bf[:], in_=lam.partition_broadcast(P))
         load_rows(0)
         load_grad(0)
-        nc.sync.dma_start(out=kap_sb[:], in_=kap_rows)
         load_grad(1)
         make_identity(nc, ident[:])
         nc.vector.memset(warm[:], 0.0)
         nc.scalar.activation(out=warm[:], in_=warm[:], func=ACT.Tanh)
         nc.vector.tensor_copy(out=lam_f[:], in_=lam_bf[:])
-        for a in range(4):
-            nc.vector.tensor_reduce(
-                out=fold[:, a * V : (a + 1) * V], in_=ident[:].rearrange("p (a v) -> p v a", v=V), axis=AX.X, op=ALU.add
-            )
-        for a in range(PV_N // V):
-            nc.vector.tensor_reduce(
-                out=fold_v[:, a * V : (a + 1) * V], in_=ident[:].rearrange("p (v a) -> p v a", v=V), axis=AX.X, op=ALU.add
-            )
+        for a in range(LONE_N // V):
+            for tile, pattern in ((fold_u, "p (a v) -> p v a"), (fold_v, "p (v a) -> p v a")):
+                nc.vector.tensor_reduce(
+                    out=tile[:, a * V : (a + 1) * V], in_=ident[:].rearrange(pattern, v=V), axis=AX.X, op=ALU.add
+                )
         turn_rows(("p", 0))
         turn_rows(("th", 0))
         take_rows(p_t, ("p", 0), False)
@@ -409,8 +402,14 @@ def tile_attgcn_pa_v_kernel(
         quantize(kap_q[:], kap_s[:], kap_g, E4)
         square(0)
         tanh(1)
-        square(1)
-        tanh(2)
+        for n in G_HEAD:
+            if n == 2:
+                tanh(2)
+            square_cols(n, 0, TOK, False)
+        if 1 not in G_HEAD:
+            square(1)
+        if 2 not in G_HEAD:
+            tanh(2)
         tanh(3)
         quant_dz2(0, HALF, TOK)
         interleave(1, 0, nc.gpsimd)
@@ -426,7 +425,7 @@ def tile_attgcn_pa_v_kernel(
             first = 4 * (4 * r - 3)
             at(first - 5, load_rows, r)
             at(first, turn_rows, ("p", r))
-            at(first + 1, take_rows, p_t, ("p", r), not ROWS_ON_V)
+            at(first + 1, take_rows, p_t, ("p", r), SCALAR_MISC)
             at(first + 2, turn_rows, ("th", r))
             at(first + 3, take_rows, th_t, ("th", r), False)
         w_g = {}
@@ -450,7 +449,7 @@ def tile_attgcn_pa_v_kernel(
             at(first, new_w, i)
             for pair in range(2):
                 at(first + 2 * pair, turn_words, w_sb[:, i, :, :], pair, ("w", i, pair))
-                at(first + 2 * pair + 1, take_w, i, pair, pair == 0 and not ROWS_ON_V)
+                at(first + 2 * pair + 1, take_w, i, pair, pair == 0 and SCALAR_MISC)
             at(first + 5, quant_w, i)
 
         def load_x(q):
@@ -463,19 +462,20 @@ def tile_attgcn_pa_v_kernel(
         def quant_x(t):
             quantize(x_q[:, t, :], x_s[:, t, :], x_il[t], E4)
 
-        for t in range(T):
-            at(4 * (6 + t) + Q_STEP, interleave_x, t)
-            at(4 * (7 + t) + Q_STEP, quant_x, t)
+        for i in range(2 * T):
+            at(4 * (5 + i) + Q_STEP, interleave_x, i)
+            if i % 2 == 1:
+                at(4 * (6 + i) + Q_STEP, quant_x, i // 2)
 
         for b in range(B):
             last = b == B - 1
             if b % 4 == 3:
                 g = b // 4
-                at(4 * b + 7, round_dp, g)
-                at(4 * b + (8 if last else 4 + Q_STEP + 4), quant_dz1, g, 0)
-                at(4 * b + (8 if last else 12 + Q_STEP), quant_dz1, g, 1)
-                at(4 * b + (8 if last else 12 + Q_STEP), product_0, g)
-                at(4 * b + (9 if last else 13 + Q_STEP), store_0, g)
+                for i in range(2):
+                    at(4 * b + (8 if last else 12 + Q_STEP), round_dz1, g, i)
+                    at(4 * b + (9 if last else 16 + Q_STEP), quant_dz1, g, i)
+                at(4 * b + (9 if last else 16 + Q_STEP), product_0, g)
+                at(4 * b + (10 if last else 17 + Q_STEP), store_0, g)
         for b in range(B):
             if b + 2 < B:
                 at(4 * b - 1, load_grad, b + 2)
@@ -493,17 +493,11 @@ def tile_attgcn_pa_v_kernel(
                 for w in PIECES:
                     at(n - 3, square_cols, n, lo, lo + w, False)
                     lo += w
-            last = b == B - 1
-            at(4 * b + (5 if last else PART_LAG), take_part, b, PART_ON_V and not last)
-            for ct in range(PACK):
-                at(4 * b + (6 if last else PART_LAG + 1 + ct), fold_part, b, ct)
-            at(4 * b + (7 if last else PART_LAG + 5), round_dt, b)
         for n in range(N_UNITS):
-            if on_tensor(n):
-                at(n + 2, sum_v_tensor, n)
-                at(n + PV_LAG, take_pv, n)
-                at(n + PV_LAG + 1, fold_pv, n)
-                at(n + PV_LAG + 2, keep_pv, n)
+            tail = n >= 60
+            at(n + (2 if tail else LAG_C), take_sums, n)
+            at(n + (3 if tail else LAG_R), fold_sums, n)
+            at(n + (4 if tail else LAG_K), keep_sums, n)
         for ct in range(PACK):
             at(N_UNITS - 3 + ct, turn_dp, ct)
             at(N_UNITS - 2 + ct, round_dpm, ct)
@@ -527,7 +521,9 @@ def tile_attgcn_pa_v_kernel(
                 weigh(s)
             if 0 <= s - 1 < N_UNITS and not on_tensor(s - 1):
                 sum_v(s - 1)
-            if 0 <= s - 2 < N_UNITS:
-                sum_u(s - 2)
+            if 0 <= s - LAG_T < 60:
+                turn_sums(s - LAG_T)
+            if 60 <= s - 1 < N_UNITS:
+                turn_sums(s - 1)
             for fn, args in side.get(s, []):
                 fn(*args)

@@ -6,43 +6,35 @@ from concourse.masks import make_identity
 B, T, V, C, K = 16, 4, 32, 512, 512
 P = 128
 PACK = 4
-TOK = V * V
-HALF = 512
-N_UNITS = B * PACK
-LEAD = 4
-F_BUFS = 4
-Q_STEP = 1
-PE_CT = (2,)
-PE_ODD = ()
-PIECES = (256, 256, 512)
-GP_COLS = 0
-WORK = 4
-TP_BUFS = 2
-V_HEAD = 3
-G_HEAD = ()
-SCALAR_TP = (0, 2)
-SCALAR_MISC = False
-LAG_T = 2
-LAG_C = 3
-LAG_R = 4
-LAG_K = 5
-FOLD_N = 128
-LONE_N = 128
-FLOPS = 2 * B * TOK * K * K + 2 * (B * V) * (2 * K) * C + 2 * T * C * (B * V) * K
+PAIRS = V * V
+BANK = 512
+UNITS = B * PACK
+ROWS = B * V
+BLOCKS = PAIRS // P
+
+FLOPS = 2 * B * PAIRS * K * K + 2 * ROWS * (2 * K) * C + 2 * T * C * ROWS * K
 BYTES = (
-    B * T * V * C * 2 + 3 * C * K * 2 + 2 * B * V * K * 4 + B * K * TOK * 2 + 2
-    + B * T * V * C * 4 + C * K * 4
+    2 * (B * T * V * C + 3 * C * K + B * K * PAIRS + 1)
+    + 4 * (2 * ROWS * K)
+    + 4 * (B * T * V * C + C * K)
 )
 
 F32 = mybir.dt.float32
 BF16 = mybir.dt.bfloat16
 U32 = mybir.dt.uint32
 U8 = mybir.dt.uint8
-E4 = mybir.dt.float8_e4m3fn_x4
-E5 = mybir.dt.float8_e5m2_x4
+E4M3 = mybir.dt.float8_e4m3fn_x4
+E5M2 = mybir.dt.float8_e5m2_x4
 ALU = mybir.AluOpType
 ACT = mybir.ActivationFunctionType
-AX = mybir.AxisListType
+AXIS = mybir.AxisListType
+
+TENSOR_SUM_CT = 2
+GPSIMD_SQUARE_CT = 3
+VECTOR_SQUARES = 2
+LATE_GPSIMD_UNITS = (61, 62)
+SCALAR_TAKES_FROM = 40
+LAST_BATCH = UNITS - PACK
 
 
 def tile_attgcn_pa_v_kernel(
@@ -51,479 +43,410 @@ def tile_attgcn_pa_v_kernel(
     nc = tc.nc
     with ExitStack() as ctx:
         keep = ctx.enter_context(tc.tile_pool(name="keep", bufs=1))
-        gin = ctx.enter_context(tc.tile_pool(name="gin", bufs=3))
-        mid = ctx.enter_context(tc.tile_pool(name="mid", bufs=3))
-        deep = ctx.enter_context(tc.tile_pool(name="deep", bufs=4))
         two = ctx.enter_context(tc.tile_pool(name="two", bufs=2))
-        work_pool = ctx.enter_context(tc.psum_pool(name="work_pool", bufs=WORK))
-        tp_pool = ctx.enter_context(tc.psum_pool(name="tp_pool", bufs=TP_BUFS))
-        rr_pool = ctx.enter_context(tc.psum_pool(name="rr_pool", bufs=8 - WORK - TP_BUFS))
-        il_pool = ctx.enter_context(tc.tile_pool(name="il_pool", bufs=1))
-        f_pool = ctx.enter_context(tc.tile_pool(name="f_pool", bufs=F_BUFS))
+        three = ctx.enter_context(tc.tile_pool(name="three", bufs=3))
+        four = ctx.enter_context(tc.tile_pool(name="four", bufs=4))
+        work_pool = ctx.enter_context(tc.psum_pool(name="work_pool", bufs=4))
+        turned_pool = ctx.enter_context(tc.psum_pool(name="turned_pool", bufs=2))
+        folded_pool = ctx.enter_context(tc.psum_pool(name="folded_pool", bufs=2))
         ctx.enter_context(tc.manual_schedule())
 
-        lam_bf = keep.tile([P, 1], BF16, name="lam_bf")
-        lam_f = keep.tile([P, 1], F32, name="lam_f")
+        lam_bf16 = keep.tile([P, 1], BF16, name="lam_bf16")
+        lam_f32 = keep.tile([P, 1], F32, name="lam_f32")
         ident = keep.tile([P, P], F32, name="ident")
-        fold_u = keep.tile([P, 2 * P], F32, name="fold_u")
-        fold_v = keep.tile([P, 2 * P], F32, name="fold_v")
-        warm = keep.tile([P, 1], F32, name="warm")
-        raw_rows = {}
-        p_t = keep.tile([P, PACK, B * V], F32, name="p_t")
-        th_t = keep.tile([P, PACK, B * V], F32, name="th_t")
-        d_t = keep.tile([P, 2, PACK, B * V], F32, name="d_t")
-        dp_t = d_t[:, 0, :, :]
-        kap_sb = keep.tile([P, PACK, K], BF16, name="kap_sb", align_bytes=64)
-        kap_q = keep.tile([P, K], U32, name="kap_q", align_bytes=64)
-        kap_s = keep.tile([P, K], U8, name="kap_s", align_bytes=64)
+        fold_u = keep.tile([P, P], F32, name="fold_u")
+        fold_v = keep.tile([P, P], F32, name="fold_v")
+        table = keep.tile([P, 1], F32, name="table")
+        p_t = keep.tile([P, PACK, ROWS], F32, name="p_t")
+        th_t = keep.tile([P, PACK, ROWS], F32, name="th_t")
+        sums = keep.tile([P, 2, PACK, ROWS], F32, name="sums")
+        kappa_sb = keep.tile([P, PACK, K], BF16, name="kappa_sb", align_bytes=64)
+        kappa_g = keep.tile([P, K, PACK], BF16, name="kappa_g", align_bytes=64)
+        kappa_q = keep.tile([P, K], U32, name="kappa_q", align_bytes=64)
+        kappa_s = keep.tile([P, K], U8, name="kappa_s", align_bytes=64)
         w_sb = keep.tile([P, 2, 4, K], BF16, name="w_sb", align_bytes=64)
         w_q = keep.tile([P, 2, C], U32, name="w_q", align_bytes=64)
         w_s = keep.tile([P, 2, C], U8, name="w_s", align_bytes=64)
         x_sb = keep.tile([P, T, PACK * C], BF16, name="x_sb", align_bytes=64)
         x_q = keep.tile([P, T, C], U32, name="x_q", align_bytes=64)
         x_s = keep.tile([P, T, C], U8, name="x_s", align_bytes=64)
-        dpm = keep.tile([P, K, PACK], BF16, name="dpm", align_bytes=64)
-        dpm_q = keep.tile([P, K], U32, name="dpm_q", align_bytes=64)
-        dpm_s = keep.tile([P, K], U8, name="dpm_s", align_bytes=64)
+        dp_g = keep.tile([P, K, PACK], BF16, name="dp_g", align_bytes=64)
+        dp_q = keep.tile([P, K], U32, name="dp_q", align_bytes=64)
+        dp_s = keep.tile([P, K], U8, name="dp_s", align_bytes=64)
 
-        p_rows = p.rearrange("b u c -> (b u) c")
-        th_rows = th.rearrange("b v c -> (b v) c")
-        kap_rows = kappa_w.rearrange("(m t) k -> m t k", t=PACK)
-        g_tiles, il_tiles, q_tiles, s_tiles = {}, {}, {}, {}
-        f_tiles, f2_tiles, df_tiles, ns_tiles = {}, {}, {}, {}
-        tp_tiles, tp_sb, rr_tiles = {}, {}, {}
-        banks = {}
+        raw, banks, grads, mixed, dz2_q, dz2_s = {}, {}, {}, {}, {}, {}
+        tanhs, squares, weighted, turned, turned_sb, folded = {}, {}, {}, {}, {}, {}
+        w_g, x_g, dz1_g, dz1_q, dz1_s = {}, {}, {}, {}, {}
 
-        def load_rows(r):
-            rows = slice(r * P, (r + 1) * P)
-            for key, src in (("p", p_rows), ("th", th_rows)):
-                raw = two.tile([P, K], F32, name="raw_" + key)
-                raw_rows[key, r] = raw
-                nc.sync.dma_start(out=raw[:], in_=src[rows, :])
-
-        def load_grad(b):
-            g = gin.tile([P, PACK, TOK], BF16, name="g", align_bytes=64)
-            g_tiles[b] = g
-            src = grad_out[b].rearrange("(p j) u v -> p j (u v)", j=PACK)
-            if b == 0:
-                for h in range(2):
-                    cols = slice(h * HALF, (h + 1) * HALF)
-                    nc.sync.dma_start(out=g[:, :, cols], in_=src[:, :, cols])
-                    if h == 0:
-                        nc.sync.dma_start(out=kap_sb[:], in_=kap_rows)
-            else:
-                nc.sync.dma_start(out=g[:], in_=src)
-
-        def turn_rows(key):
-            bank = work_pool.tile([P, HALF], F32, name="bank", tag="work")
+        def new_bank(key):
+            bank = work_pool.tile([P, BANK], F32, name="bank")
             banks[key] = bank
-            for t in range(PACK):
-                nc.tensor.transpose(bank[:, t * P : (t + 1) * P], raw_rows[key][:, t:K:PACK], ident[:])
-
-        def take_rows(dst, key, on_scalar):
-            r = key[1]
-            src = banks[key][:].rearrange("p (t q) -> p t q", t=PACK)
-            out = dst[:, :, r * P : (r + 1) * P]
-            if on_scalar:
-                nc.scalar.copy(out=out, in_=src)
-            else:
-                nc.vector.tensor_copy(out=out, in_=src)
-
-        def turn_words(sb, pair, key):
-            bank = work_pool.tile([P, HALF], F32, name="bank", tag="work")
-            banks[key] = bank
-            for i in range(2):
-                words = sb[:, 2 * pair + i, :].bitcast(F32)
-                for u in range(2):
-                    at = (2 * i + u) * P
-                    nc.tensor.transpose(bank[:, at : at + P], words[:, u : K // 2 : 2], ident[:])
-
-        def take_words(grouped, pair, key, on_scalar):
-            src = banks[key][:].rearrange("p (i u m) -> p i m u", i=2, u=2)
-            flat = grouped[:].rearrange("p c t -> p (c t)").bitcast(F32)
-            out = flat[:, pair * 512 : (pair + 1) * 512].rearrange("p (i m u) -> p i m u", i=2, u=2)
-            if on_scalar:
-                nc.scalar.copy(out=out, in_=src)
-            else:
-                nc.vector.tensor_copy(out=out, in_=src)
+            return bank
 
         def quantize(codes, scales, grouped, fmt):
             nc.vector.quantize_mx(
                 out=codes.bitcast(fmt), scales=scales, in_=grouped[:].rearrange("p c t -> p (c t)")
             )
 
-        def interleave(b, h, engine):
-            if h == 0:
-                il_tiles[b] = il_pool.tile([P, TOK, PACK], BF16, name="il", align_bytes=64)
-            cols = slice(h * HALF, (h + 1) * HALF)
+        def load_rows(r):
+            for name, src in (("p", p), ("th", th)):
+                tile = two.tile([P, K], F32, name="raw_" + name)
+                raw[name, r] = tile
+                nc.sync.dma_start(out=tile[:], in_=src.rearrange("b j c -> (b j) c")[r * P : (r + 1) * P, :])
+
+        def turn_rows(name, r):
+            bank = new_bank((name, r))
+            for t in range(PACK):
+                nc.tensor.transpose(bank[:, t * P : (t + 1) * P], raw[name, r][:, t:K:PACK], ident[:])
+
+        def take_rows(name, r):
+            src = banks[name, r][:].rearrange("p (t q) -> p t q", t=PACK)
+            dst = (p_t if name == "p" else th_t)[:, :, r * P : (r + 1) * P]
+            if (name, r) == ("th", 0):
+                nc.scalar.copy(out=dst, in_=src)
+            else:
+                nc.vector.tensor_copy(out=dst, in_=src)
+
+        def turn_weight(weight, half, key):
+            bank = new_bank(key)
+            for i in range(2):
+                pairs_of_k = weight[:, 2 * half + i, :].bitcast(F32)
+                for u in range(2):
+                    col = (2 * i + u) * P
+                    nc.tensor.transpose(bank[:, col : col + P], pairs_of_k[:, u : K // 2 : 2], ident[:])
+
+        def take_weight(grouped, half, key):
+            src = banks[key][:].rearrange("p (i u m) -> p i m u", i=2, u=2)
+            flat = grouped[:].rearrange("p c t -> p (c t)").bitcast(F32)
+            dst = flat[:, half * BANK : (half + 1) * BANK].rearrange("p (i m u) -> p i m u", i=2, u=2)
+            nc.vector.tensor_copy(out=dst, in_=src)
+
+        def load_grad(b):
+            tile = three.tile([P, PACK, PAIRS], BF16, name="grad", align_bytes=64)
+            grads[b] = tile
+            nc.sync.dma_start(out=tile[:], in_=grad_out[b].rearrange("(p j) u v -> p j (u v)", j=PACK))
+
+        def mix(b, half, engine):
+            if half == 0:
+                mixed[b] = keep.tile([P, PAIRS, PACK], BF16, name="mixed", align_bytes=64)
+            cols = slice(half * BANK, (half + 1) * BANK)
             engine.tensor_scalar(
-                out=il_tiles[b][:, cols, :], in0=g_tiles[b][:, :, cols].rearrange("p j n -> p n j"),
-                scalar1=lam_f[:, 0:1], scalar2=0.0, op0=ALU.mult, op1=ALU.add,
+                out=mixed[b][:, cols, :], in0=grads[b][:, :, cols].rearrange("p j n -> p n j"),
+                scalar1=lam_f32[:, 0:1], scalar2=0.0, op0=ALU.mult, op1=ALU.add,
             )
 
-        def quant_dz2(b, lo, hi):
+        def quantize_dz2(b, lo, hi):
             if lo == 0:
-                q_tiles[b] = mid.tile([P, TOK], U32, name="dz2_q", align_bytes=64)
-                s_tiles[b] = mid.tile([P, TOK], U8, name="dz2_s", align_bytes=64)
+                dz2_q[b] = three.tile([P, PAIRS], U32, name="dz2_q", align_bytes=64)
+                dz2_s[b] = three.tile([P, PAIRS], U8, name="dz2_s", align_bytes=64)
             cols = slice(lo, hi)
-            quantize(q_tiles[b][:, cols], s_tiles[b][:, cols], il_tiles[b][:, cols, :], E5)
+            quantize(dz2_q[b][:, cols], dz2_s[b][:, cols], mixed[b][:, cols, :], E5M2)
 
         def tanh(n):
             b, ct = divmod(n, PACK)
-            f = f_pool.tile([P, TOK], F32, name="f")
-            f_tiles[n] = f
+            tile = four.tile([P, PAIRS], F32, name="f")
+            tanhs[n] = tile
             for u in range(V):
-                col = b * V + u
+                row = b * V + u
                 nc.scalar.activation(
-                    out=f[:, u * V : (u + 1) * V],
-                    in_=th_t[:, ct, b * V : (b + 1) * V],
-                    func=ACT.Tanh,
-                    bias=p_t[:, ct, col : col + 1],
-                    scale=-1.0,
+                    out=tile[:, u * V : (u + 1) * V], in_=th_t[:, ct, b * V : (b + 1) * V], func=ACT.Tanh,
+                    bias=p_t[:, ct, row : row + 1], scale=-1.0,
                 )
 
-        def square_cols(n, lo, hi, on_scalar):
-            if n not in f2_tiles:
-                f2_tiles[n] = deep.tile([P, TOK], F32, name="f2")
-            f2, f = f2_tiles[n], f_tiles[n]
-            if on_scalar:
-                nc.scalar.activation(out=f2[:, lo:hi], in_=f[:, lo:hi], func=ACT.Square)
-            else:
-                nc.gpsimd.tensor_tensor(out=f2[:, lo:hi], in0=f[:, lo:hi], in1=f[:, lo:hi], op=ALU.mult)
-
-        def gp_share(n):
-            if n in G_HEAD:
-                return TOK
-            if n < 7:
-                return 0
-            if n >= 61 or n % 4 == 3:
-                return sum(PIECES)
-            return GP_COLS if n % 4 == 2 else 0
+        def on_gpsimd(n):
+            return (n % PACK == GPSIMD_SQUARE_CT and n >= 2 * PACK - 1) or n in LATE_GPSIMD_UNITS
 
         def square(n):
-            g = gp_share(n)
-            if n < V_HEAD:
-                f2_tiles[n] = deep.tile([P, TOK], F32, name="f2")
-                nc.vector.tensor_tensor(out=f2_tiles[n][:], in0=f_tiles[n][:], in1=f_tiles[n][:], op=ALU.mult)
-            elif g < TOK:
-                square_cols(n, g, TOK, True)
+            tile = four.tile([P, PAIRS], F32, name="f_squared")
+            squares[n] = tile
+            f = tanhs[n]
+            if on_gpsimd(n):
+                nc.gpsimd.tensor_tensor(out=tile[:], in0=f[:], in1=f[:], op=ALU.mult)
+            elif n < VECTOR_SQUARES:
+                nc.vector.tensor_tensor(out=tile[:], in0=f[:], in1=f[:], op=ALU.mult)
+            else:
+                nc.scalar.activation(out=tile[:], in_=f[:], func=ACT.Square)
 
         def multiply(n):
             b, ct = divmod(n, PACK)
-            w_cols = slice(ct * P, (ct + 1) * P)
-            for h in range(2):
-                cols = slice(h * HALF, (h + 1) * HALF)
-                df = work_pool.tile([P, HALF], F32, name="df", tag="work")
-                df_tiles[n, h] = df
+            channels = slice(ct * P, (ct + 1) * P)
+            for half in range(2):
+                cols = slice(half * BANK, (half + 1) * BANK)
+                bank = new_bank((n, half))
                 nc.tensor.matmul_mx(
-                    out=df[:],
-                    lhsT=kap_q[:, w_cols].bitcast(E4),
-                    lhsT_scale=kap_s[:, w_cols],
-                    rhs=q_tiles[b][:, cols].bitcast(E5),
-                    rhs_scale=s_tiles[b][:, cols],
-                    start=True,
-                    stop=True,
+                    out=bank[:], lhsT=kappa_q[:, channels].bitcast(E4M3), lhsT_scale=kappa_s[:, channels],
+                    rhs=dz2_q[b][:, cols].bitcast(E5M2), rhs_scale=dz2_s[b][:, cols], start=True, stop=True,
                 )
 
         def weigh(n):
-            ns = deep.tile([P, TOK], F32, name="ns")
-            ns_tiles[n] = ns
-            for h in range(2):
-                cols = slice(h * HALF, (h + 1) * HALF)
+            tile = four.tile([P, PAIRS], F32, name="minus_ds")
+            weighted[n] = tile
+            for half in range(2):
+                cols = slice(half * BANK, (half + 1) * BANK)
                 nc.vector.scalar_tensor_tensor(
-                    out=ns[:, cols], in0=f2_tiles[n][:, cols], scalar=1.0, in1=df_tiles[n, h][:],
+                    out=tile[:, cols], in0=squares[n][:, cols], scalar=1.0, in1=banks[n, half][:],
                     op0=ALU.subtract, op1=ALU.mult,
                 )
 
-        def sum_v(n):
+        def tensor_sums_v(n):
+            return n % PACK == TENSOR_SUM_CT and n < LAST_BATCH
+
+        def sum_over_v(n):
             b, ct = divmod(n, PACK)
             nc.vector.tensor_reduce(
-                out=dp_t[:, ct, b * V : (b + 1) * V],
-                in_=ns_tiles[n][:].rearrange("p (u v) -> p u v", v=V),
-                axis=AX.X,
-                op=ALU.add,
+                out=sums[:, 0, ct, b * V : (b + 1) * V],
+                in_=weighted[n][:].rearrange("p (u v) -> p u v", v=V), axis=AXIS.X, op=ALU.add,
             )
 
-        def on_tensor(n):
-            return (n % PACK in PE_CT or (n % 8 in PE_ODD)) and n < N_UNITS - PACK
-
         def turn_sums(n):
-            tp_tiles[n] = tp_pool.tile([P, 2 * P], F32, name="tp")
-            ns = ns_tiles[n]
-            for i in range(8):
+            tile = turned_pool.tile([P, 2 * P], F32, name="turned")
+            turned[n] = tile
+            src = weighted[n]
+            for i in range(BLOCKS):
                 nc.tensor.matmul(
-                    tp_tiles[n][:, 0:P], ns[:, i * P : (i + 1) * P], ident[:],
-                    start=(i == 0), stop=(i == 7), is_transpose=True,
+                    tile[:, 0:P], src[:, i * P : (i + 1) * P], ident[:],
+                    start=(i == 0), stop=(i == BLOCKS - 1), is_transpose=True,
                 )
-            if on_tensor(n):
-                for i in range(8):
+            if tensor_sums_v(n):
+                for r in range(BLOCKS):
                     nc.tensor.matmul(
-                        tp_tiles[n][:, P : 2 * P], ns[:, i:TOK:8], ident[:],
-                        start=(i == 0), stop=(i == 7), is_transpose=True,
+                        tile[:, P : 2 * P], src[:, r:PAIRS:BLOCKS], ident[:],
+                        start=(r == 0), stop=(r == BLOCKS - 1), is_transpose=True,
                     )
 
-        def width(n):
-            return 2 if on_tensor(n) else 1
-
         def take_sums(n):
-            tp_sb[n] = mid.tile([P, 2 * P], F32, name="tp_sb")
-            cols = slice(0, width(n) * P)
-            if n % PACK in SCALAR_TP or n >= 60:
-                nc.scalar.copy(out=tp_sb[n][:, cols], in_=tp_tiles[n][:, cols])
+            tile = three.tile([P, 2 * P], F32, name="turned_sb")
+            turned_sb[n] = tile
+            cols = slice(0, 2 * P if tensor_sums_v(n) else P)
+            if n >= SCALAR_TAKES_FROM:
+                nc.scalar.copy(out=tile[:, cols], in_=turned[n][:, cols])
             else:
-                nc.vector.tensor_copy(out=tp_sb[n][:, cols], in_=tp_tiles[n][:, cols])
+                nc.vector.tensor_copy(out=tile[:, cols], in_=turned[n][:, cols])
 
         def fold_sums(n):
-            rr_tiles[n] = rr_pool.tile([P, 2 * P], F32, name="rr")
-            for i in range(width(n)):
-                wide = FOLD_N if width(n) == 2 else LONE_N
-                cols = slice(i * P, i * P + wide)
-                nc.tensor.matmul(
-                    rr_tiles[n][:, cols], tp_sb[n][:, i * P : (i + 1) * P], (fold_u, fold_v)[i][:, 0:wide],
-                    start=True, stop=True,
-                )
+            tile = folded_pool.tile([P, 2 * P], F32, name="folded")
+            folded[n] = tile
+            for i, matrix in enumerate((fold_u, fold_v) if tensor_sums_v(n) else (fold_u,)):
+                cols = slice(i * P, (i + 1) * P)
+                nc.tensor.matmul(tile[:, cols], turned_sb[n][:, cols], matrix[:], start=True, stop=True)
 
         def keep_sums(n):
             b, ct = divmod(n, PACK)
-            cols = slice(b * V, (b + 1) * V)
-            if on_tensor(n):
-                nc.vector.tensor_copy(out=d_t[:, 0, ct, cols], in_=rr_tiles[n][:, P : P + V])
-            if n >= 60:
-                nc.scalar.copy(out=d_t[:, 1, ct, cols], in_=rr_tiles[n][:, 0:V])
+            rows = slice(b * V, (b + 1) * V)
+            if tensor_sums_v(n):
+                nc.vector.tensor_copy(out=sums[:, 0, ct, rows], in_=folded[n][:, P : P + V])
+            if n >= LAST_BATCH:
+                nc.scalar.copy(out=sums[:, 1, ct, rows], in_=folded[n][:, 0:V])
             else:
-                nc.vector.tensor_copy(out=d_t[:, 1, ct, cols], in_=rr_tiles[n][:, 0:V])
+                nc.vector.tensor_copy(out=sums[:, 1, ct, rows], in_=folded[n][:, 0:V])
 
-        dz1 = {}
-
-        def round_dz1(g, i):
-            grouped = two.tile([P, P, PACK], BF16, name="dz1_g%d" % i, align_bytes=64)
-            dz1[g, i] = grouped
-            src = d_t[:, i, :, g * P : (g + 1) * P].rearrange("p t n -> p n t")
-            factor = (-0.25, 0.25)[i]
-            if SCALAR_MISC or g == 3:
-                nc.scalar.activation(out=grouped[:], in_=src, func=ACT.Copy, scale=factor)
+        def round_dz1(g, part):
+            tile = two.tile([P, P, PACK], BF16, name="dz1_g%d" % part, align_bytes=64)
+            dz1_g[g, part] = tile
+            src = sums[:, part, :, g * P : (g + 1) * P].rearrange("p t n -> p n t")
+            factor = (-0.25, 0.25)[part]
+            if g == 3:
+                nc.scalar.activation(out=tile[:], in_=src, func=ACT.Copy, scale=factor)
             else:
-                nc.vector.tensor_scalar(out=grouped[:], in0=src, scalar1=factor, scalar2=None, op0=ALU.mult)
+                nc.vector.tensor_scalar(out=tile[:], in0=src, scalar1=factor, scalar2=None, op0=ALU.mult)
 
-        dz1_q = {}
+        def quantize_dz1(g, part):
+            dz1_q[g, part] = two.tile([P, P], U32, name="dz1_q%d" % part, align_bytes=64)
+            dz1_s[g, part] = two.tile([P, P], U8, name="dz1_s%d" % part, align_bytes=64)
+            quantize(dz1_q[g, part][:], dz1_s[g, part][:], dz1_g[g, part], E5M2)
 
-        def quant_dz1(g, i):
-            codes = two.tile([P, P], U32, name="dz1_q%d" % i, align_bytes=64)
-            scales = two.tile([P, P], U8, name="dz1_s%d" % i, align_bytes=64)
-            dz1_q[g, i] = (codes, scales)
-            quantize(codes[:], scales[:], dz1[g, i], E5)
-
-        def product_0(g):
-            bank = work_pool.tile([P, HALF], F32, name="bank", tag="work")
-            banks["o0", g] = bank
-            for i in range(2):
-                codes, scales = dz1_q[g, i]
+        def multiply_out_0(g):
+            bank = new_bank(("out_0", g))
+            for part in range(2):
                 nc.tensor.matmul_mx(
-                    out=bank[:], lhsT=codes[:].bitcast(E5), lhsT_scale=scales[:],
-                    rhs=w_q[:, i, :].bitcast(E4), rhs_scale=w_s[:, i, :],
-                    start=(i == 0), stop=(i == 1),
+                    out=bank[:], lhsT=dz1_q[g, part][:].bitcast(E5M2), lhsT_scale=dz1_s[g, part][:],
+                    rhs=w_q[:, part, :].bitcast(E4M3), rhs_scale=w_s[:, part, :],
+                    start=(part == 0), stop=(part == 1),
                 )
 
-        def store_0(g):
-            rows = two.tile([P, C], F32, name="rows")
-            if not SCALAR_MISC and g < 3:
-                nc.vector.tensor_copy(out=rows[:], in_=banks["o0", g][:])
+        def store_out_0(g):
+            tile = two.tile([P, C], F32, name="out_0_rows")
+            if g < 2:
+                nc.vector.tensor_copy(out=tile[:], in_=banks["out_0", g][:])
             else:
-                nc.scalar.copy(out=rows[:], in_=banks["o0", g][:])
+                nc.scalar.copy(out=tile[:], in_=banks["out_0", g][:])
             for i in range(4):
-                src = rows[i * V : (i + 1) * V, :].unsqueeze(1).to_broadcast([V, T, C])
+                src = tile[i * V : (i + 1) * V, :].unsqueeze(1).to_broadcast([V, T, C])
                 nc.sync.dma_start(out=out_0[4 * g + i].rearrange("t j c -> j t c"), in_=src)
-
-        x_il = {}
-
-        def interleave_x(i):
-            t, h = divmod(i, 2)
-            if h == 0:
-                x_il[t] = two.tile([P, C, PACK], BF16, name="x_il", align_bytes=64)
-            cols = slice(h * C // 2, (h + 1) * C // 2)
-            src = x_sb[:, t, :].rearrange("p (j c) -> p c j", j=PACK)[:, cols, :]
-            nc.vector.tensor_copy(out=x_il[t][:, cols, :], in_=src)
-
-        def turn_dp(ct):
-            bank = work_pool.tile([P, HALF], F32, name="bank", tag="work")
-            banks["dp", ct] = bank
-            for t in range(PACK):
-                nc.tensor.transpose(bank[:, t * P : (t + 1) * P], dp_t[:, ct, t : B * V : PACK], ident[:])
-
-        def round_dpm(ct):
-            nc.scalar.activation(
-                out=dpm[:, ct * P : (ct + 1) * P, :],
-                in_=banks["dp", ct][:].rearrange("p (t m) -> p m t", t=PACK), func=ACT.Copy, scale=-0.25,
-            )
-
-        def product_1(m):
-            bank = work_pool.tile([P, HALF], F32, name="bank", tag="work")
-            rows = slice(m * P, (m + 1) * P)
-            for t in range(T):
-                nc.tensor.matmul_mx(
-                    out=bank[:], lhsT=x_q[:, t, rows].bitcast(E4), lhsT_scale=x_s[:, t, rows],
-                    rhs=dpm_q[:].bitcast(E5), rhs_scale=dpm_s[:], start=(t == 0), stop=(t == T - 1),
-                )
-            o = deep.tile([P, K], F32, name="o1")
-            src = bank[:].rearrange("p (t m) -> p m t", t=PACK)
-            dst = o[:].rearrange("p (m t) -> p m t", t=PACK)
-            if m % 2 == 0:
-                nc.vector.tensor_copy(out=dst, in_=src)
-            else:
-                nc.scalar.copy(out=dst, in_=src)
-            nc.sync.dma_start(out=out_1[rows, :], in_=o[:])
-
-        nc.scalar.dma_start(out=lam_bf[:], in_=lam.partition_broadcast(P))
-        load_rows(0)
-        load_grad(0)
-        load_grad(1)
-        make_identity(nc, ident[:])
-        nc.vector.memset(warm[:], 0.0)
-        nc.scalar.activation(out=warm[:], in_=warm[:], func=ACT.Tanh)
-        nc.vector.tensor_copy(out=lam_f[:], in_=lam_bf[:])
-        for a in range(LONE_N // V):
-            for tile, pattern in ((fold_u, "p (a v) -> p v a"), (fold_v, "p (v a) -> p v a")):
-                nc.vector.tensor_reduce(
-                    out=tile[:, a * V : (a + 1) * V], in_=ident[:].rearrange(pattern, v=V), axis=AX.X, op=ALU.add
-                )
-        turn_rows(("p", 0))
-        turn_rows(("th", 0))
-        take_rows(p_t, ("p", 0), False)
-        take_rows(th_t, ("th", 0), True)
-        kap_g = keep.tile([P, K, PACK], BF16, name="kap_g", align_bytes=64)
-        turn_words(kap_sb, 0, "k0")
-        turn_words(kap_sb, 1, "k1")
-        interleave(0, 0, nc.vector)
-        interleave(0, 1, nc.gpsimd)
-        tanh(0)
-        take_words(kap_g, 0, "k0", False)
-        take_words(kap_g, 1, "k1", False)
-        quant_dz2(0, 0, HALF)
-        quantize(kap_q[:], kap_s[:], kap_g, E4)
-        square(0)
-        tanh(1)
-        for n in G_HEAD:
-            if n == 2:
-                tanh(2)
-            square_cols(n, 0, TOK, False)
-        if 1 not in G_HEAD:
-            square(1)
-        if 2 not in G_HEAD:
-            tanh(2)
-        tanh(3)
-        quant_dz2(0, HALF, TOK)
-        interleave(1, 0, nc.gpsimd)
-        interleave(1, 1, nc.gpsimd)
-        multiply(0)
-
-        side = {}
-
-        def at(step, fn, *args):
-            side.setdefault(step, []).append((fn, args))
-
-        for r in range(1, 4):
-            first = 4 * (4 * r - 3)
-            at(first - 5, load_rows, r)
-            at(first, turn_rows, ("p", r))
-            at(first + 1, take_rows, p_t, ("p", r), SCALAR_MISC)
-            at(first + 2, turn_rows, ("th", r))
-            at(first + 3, take_rows, th_t, ("th", r), False)
-        w_g = {}
 
         def load_weights():
             for i, w in enumerate((phi_w, theta_w)):
                 nc.sync.dma_start(out=w_sb[:, i, :, :], in_=w.rearrange("(r m) k -> m r k", m=P))
 
-        def new_w(i):
-            w_g[i] = two.tile([P, C, PACK], BF16, name="w_g", align_bytes=64)
+        def turn_w(i, half):
+            if half == 0:
+                w_g[i] = two.tile([P, C, PACK], BF16, name="w_g", align_bytes=64)
+            turn_weight(w_sb[:, i, :, :], half, ("w", i, half))
 
-        def take_w(i, pair, on_scalar):
-            take_words(w_g[i], pair, ("w", i, pair), on_scalar)
+        def take_w(i, half):
+            take_weight(w_g[i], half, ("w", i, half))
 
-        def quant_w(i):
-            quantize(w_q[:, i, :], w_s[:, i, :], w_g[i], E4)
+        def quantize_w(i):
+            quantize(w_q[:, i, :], w_s[:, i, :], w_g[i], E4M3)
 
-        at(2, load_weights)
+        def load_x(b):
+            src = x[b].rearrange("t (q j) c -> q t (j c)", j=PACK)
+            nc.sync.dma_start(out=x_sb[8 * b : 8 * b + 8, :, :], in_=src)
+
+        def mix_x(t, half):
+            if half == 0:
+                x_g[t] = two.tile([P, C, PACK], BF16, name="x_g", align_bytes=64)
+            cols = slice(half * C // 2, (half + 1) * C // 2)
+            src = x_sb[:, t, :].rearrange("p (j c) -> p c j", j=PACK)
+            nc.vector.tensor_copy(out=x_g[t][:, cols, :], in_=src[:, cols, :])
+
+        def quantize_x(t):
+            quantize(x_q[:, t, :], x_s[:, t, :], x_g[t], E4M3)
+
+        def turn_dp(ct):
+            bank = new_bank(("dp", ct))
+            for t in range(PACK):
+                nc.tensor.transpose(bank[:, t * P : (t + 1) * P], sums[:, 0, ct, t:ROWS:PACK], ident[:])
+
+        def round_dp(ct):
+            nc.scalar.activation(
+                out=dp_g[:, ct * P : (ct + 1) * P, :],
+                in_=banks["dp", ct][:].rearrange("p (t m) -> p m t", t=PACK), func=ACT.Copy, scale=-0.25,
+            )
+
+        def quantize_dp(ct):
+            cols = slice(ct * P, (ct + 1) * P)
+            quantize(dp_q[:, cols], dp_s[:, cols], dp_g[:, cols, :], E5M2)
+
+        def out_1_rows(i):
+            rows = slice(i * P, (i + 1) * P)
+            bank = new_bank(("out_1", i))
+            for t in range(T):
+                nc.tensor.matmul_mx(
+                    out=bank[:], lhsT=x_q[:, t, rows].bitcast(E4M3), lhsT_scale=x_s[:, t, rows],
+                    rhs=dp_q[:].bitcast(E5M2), rhs_scale=dp_s[:], start=(t == 0), stop=(t == T - 1),
+                )
+            tile = four.tile([P, K], F32, name="out_1_rows")
+            src = bank[:].rearrange("p (t m) -> p m t", t=PACK)
+            dst = tile[:].rearrange("p (m t) -> p m t", t=PACK)
+            if i % 2 == 0:
+                nc.vector.tensor_copy(out=dst, in_=src)
+            else:
+                nc.scalar.copy(out=dst, in_=src)
+            nc.sync.dma_start(out=out_1[rows, :], in_=tile[:])
+
+        nc.scalar.dma_start(out=lam_bf16[:], in_=lam.partition_broadcast(P))
+        load_rows(0)
+        grads[0] = three.tile([P, PACK, PAIRS], BF16, name="grad", align_bytes=64)
+        first_grad = grad_out[0].rearrange("(p j) u v -> p j (u v)", j=PACK)
+        nc.sync.dma_start(out=grads[0][:, :, 0:BANK], in_=first_grad[:, :, 0:BANK])
+        nc.sync.dma_start(out=kappa_sb[:], in_=kappa_w.rearrange("(m t) k -> m t k", t=PACK))
+        nc.sync.dma_start(out=grads[0][:, :, BANK:PAIRS], in_=first_grad[:, :, BANK:PAIRS])
+        load_grad(1)
+        load_rows(1)
+        load_grad(2)
+        make_identity(nc, ident[:])
+        nc.vector.memset(table[:], 0.0)
+        nc.scalar.activation(out=table[:], in_=table[:], func=ACT.Tanh)
+        for c in range(P // V):
+            for matrix, pattern in ((fold_u, "p (a v) -> p v a"), (fold_v, "p (v a) -> p v a")):
+                nc.vector.tensor_reduce(
+                    out=matrix[:, c * V : (c + 1) * V], in_=ident[:].rearrange(pattern, v=V), axis=AXIS.X, op=ALU.add
+                )
+        turn_rows("p", 0)
+        turn_rows("th", 0)
+        take_rows("p", 0)
+        take_rows("th", 0)
+        turn_weight(kappa_sb, 0, ("kappa", 0))
+        turn_weight(kappa_sb, 1, ("kappa", 1))
+        nc.vector.tensor_copy(out=lam_f32[:], in_=lam_bf16[:])
+        mix(0, 0, nc.vector)
+        mix(0, 1, nc.gpsimd)
+        tanh(0)
+        take_weight(kappa_g, 0, ("kappa", 0))
+        take_weight(kappa_g, 1, ("kappa", 1))
+        quantize_dz2(0, 0, BANK)
+        quantize(kappa_q[:], kappa_s[:], kappa_g, E4M3)
+        quantize_dz2(0, BANK, PAIRS)
+        square(0)
+        tanh(1)
+        square(1)
+        tanh(2)
+        tanh(3)
+        mix(1, 0, nc.gpsimd)
+        mix(1, 1, nc.gpsimd)
+        multiply(0)
+
+        beside = {}
+
+        def at(step, function, *arguments):
+            beside.setdefault(step, []).append((function, arguments))
+
+        for r in range(1, 4):
+            first = 16 * r - 12
+            if r > 1:
+                at(first - 10, load_rows, r)
+            for i, name in enumerate(("p", "th")):
+                at(first + 2 * i, turn_rows, name, r)
+                at(first + 2 * i + 1, take_rows, name, r)
+        at(0, load_weights)
         for i in range(2):
             first = 8 + 4 * i
-            at(first, new_w, i)
-            for pair in range(2):
-                at(first + 2 * pair, turn_words, w_sb[:, i, :, :], pair, ("w", i, pair))
-                at(first + 2 * pair + 1, take_w, i, pair, pair == 0 and SCALAR_MISC)
-            at(first + 5, quant_w, i)
-
-        def load_x(q):
-            src = x[:, :, q * PACK : (q + 1) * PACK, :].rearrange("b t j c -> b t (j c)")
-            nc.sync.dma_start(out=x_sb[q : P : 8, :, :], in_=src)
-
-        for q in range(8):
-            at(13 + q, load_x, q)
-
-        def quant_x(t):
-            quantize(x_q[:, t, :], x_s[:, t, :], x_il[t], E4)
-
-        for i in range(2 * T):
-            at(4 * (5 + i) + Q_STEP, interleave_x, i)
-            if i % 2 == 1:
-                at(4 * (6 + i) + Q_STEP, quant_x, i // 2)
-
+            for half in range(2):
+                at(first + 2 * half, turn_w, i, half)
+                at(first + 2 * half + 1, take_w, i, half)
+            at(first + 5, quantize_w, i)
         for b in range(B):
-            last = b == B - 1
-            if b % 4 == 3:
-                g = b // 4
-                for i in range(2):
-                    at(4 * b + (8 if last else 12 + Q_STEP), round_dz1, g, i)
-                    at(4 * b + (9 if last else 16 + Q_STEP), quant_dz1, g, i)
-                at(4 * b + (9 if last else 16 + Q_STEP), product_0, g)
-                at(4 * b + (10 if last else 17 + Q_STEP), store_0, g)
+            at(9 + b, load_x, b)
+        for t in range(T):
+            for half in range(2):
+                at(29 + 8 * t + 4 * half, mix_x, t, half)
+            at(37 + 8 * t, quantize_x, t)
+        for g in range(4):
+            done = 16 * g + 12
+            late = g == 3
+            for part in range(2):
+                at(done + (8 if late else 13), round_dz1, g, part)
+                at(done + (9 if late else 17), quantize_dz1, g, part)
+            at(done + (9 if late else 17), multiply_out_0, g)
+            at(done + (10 if late else 18), store_out_0, g)
         for b in range(B):
-            if b + 2 < B:
-                at(4 * b - 1, load_grad, b + 2)
+            if 3 <= b + 2 < B:
+                at(4 * b - 4, load_grad, b + 2)
             if b + 1 < B:
-                at(4 * b + Q_STEP, quant_dz2, b + 1, 0, TOK)
+                at(4 * b + 1, quantize_dz2, b + 1, 0, PAIRS)
             if b + 2 < B:
-                at(4 * b + Q_STEP + 1, interleave, b + 2, 0, nc.gpsimd)
-            n = 4 * b + 6
-            if 7 <= n < N_UNITS and gp_share(n):
-                at(4 * b + 3, square_cols, n, 0, gp_share(n), False)
-            if b + 2 < B:
-                at(4 * b + Q_STEP + 1, interleave, b + 2, 1, nc.gpsimd)
-            for n in (4 * b + 7,) if b < 14 else (61, 62, 63) if b == 14 else ():
-                lo = 0
-                for w in PIECES:
-                    at(n - 3, square_cols, n, lo, lo + w, False)
-                    lo += w
-        for n in range(N_UNITS):
-            tail = n >= 60
-            at(n + (2 if tail else LAG_C), take_sums, n)
-            at(n + (3 if tail else LAG_R), fold_sums, n)
-            at(n + (4 if tail else LAG_K), keep_sums, n)
+                at(4 * b + 2, mix, b + 2, 0, nc.gpsimd)
+                at(4 * b + 2, mix, b + 2, 1, nc.gpsimd)
+        for n in range(UNITS):
+            if on_gpsimd(n):
+                at(n - 3, square, n)
+        for n in range(UNITS):
+            late = n >= LAST_BATCH
+            at(n + (2 if late else 3), take_sums, n)
+            at(n + (3 if late else 4), fold_sums, n)
+            at(n + (4 if late else 5), keep_sums, n)
         for ct in range(PACK):
-            at(N_UNITS - 3 + ct, turn_dp, ct)
-            at(N_UNITS - 2 + ct, round_dpm, ct)
+            at(LAST_BATCH + ct + 1, turn_dp, ct)
+            at(LAST_BATCH + ct + 2, round_dp, ct)
+            at(LAST_BATCH + ct + 3, quantize_dp, ct)
+        for i in range(4):
+            at(UNITS + 5 + i, out_1_rows, i)
 
-        def quant_dpm():
-            quantize(dpm_q[:], dpm_s[:], dpm, E5)
-
-        at(N_UNITS + 2, quant_dpm)
-        for m in range(4):
-            at(N_UNITS + 3 + m, product_1, m)
-
-
-        for s in range(-1, N_UNITS + 10):
-            if 4 <= s + LEAD < N_UNITS:
-                tanh(s + LEAD)
-            if 2 <= s + 2 < N_UNITS:
+        for s in range(UNITS + 10):
+            if s + 4 < UNITS:
+                tanh(s + 4)
+            if s + 2 < UNITS and not on_gpsimd(s + 2):
                 square(s + 2)
-            if 1 <= s + 1 < N_UNITS:
+            if s + 1 < UNITS:
                 multiply(s + 1)
-            if 0 <= s < N_UNITS:
+            if s < UNITS:
                 weigh(s)
-            if 0 <= s - 1 < N_UNITS and not on_tensor(s - 1):
-                sum_v(s - 1)
-            if 0 <= s - LAG_T < 60:
-                turn_sums(s - LAG_T)
-            if 60 <= s - 1 < N_UNITS:
+            if 0 <= s - 1 < UNITS and not tensor_sums_v(s - 1):
+                sum_over_v(s - 1)
+            if 0 <= s - 2 < LAST_BATCH:
+                turn_sums(s - 2)
+            if LAST_BATCH <= s - 1 < UNITS:
                 turn_sums(s - 1)
-            for fn, args in side.get(s, []):
-                fn(*args)
+            for function, arguments in beside.get(s, []):
+                function(*arguments)

from contextlib import ExitStack

import concourse.mybir as mybir
from concourse.masks import make_identity

B, T, V, C, K = 16, 4, 32, 512, 512
P = 128
PACK = 4
PAIRS = V * V
BANK = 512
UNITS = B * PACK
ROWS = B * V
BLOCKS = PAIRS // P

FLOPS = 2 * B * PAIRS * K * K + 2 * ROWS * (2 * K) * C + 2 * T * C * ROWS * K
BYTES = (
    2 * (B * T * V * C + 3 * C * K + B * K * PAIRS + 1)
    + 4 * (2 * ROWS * K)
    + 4 * (B * T * V * C + C * K)
)

F32 = mybir.dt.float32
BF16 = mybir.dt.bfloat16
U32 = mybir.dt.uint32
U8 = mybir.dt.uint8
E4M3 = mybir.dt.float8_e4m3fn_x4
E5M2 = mybir.dt.float8_e5m2_x4
ALU = mybir.AluOpType
ACT = mybir.ActivationFunctionType
AXIS = mybir.AxisListType

TENSOR_SUM_CT = 2
GPSIMD_SQUARE_CT = 3
VECTOR_SQUARES = 2
LATE_GPSIMD_UNITS = (61, 62)
SCALAR_TAKES_FROM = 40
LAST_BATCH = UNITS - PACK


def tile_attgcn_pa_v_kernel(
    tc, x, A, lam, phi_w, phi_b, theta_w, theta_b, kappa_w, kappa_b, p, th, grad_out, out_0, out_1
):
    nc = tc.nc
    with ExitStack() as ctx:
        keep = ctx.enter_context(tc.tile_pool(name="keep", bufs=1))
        two = ctx.enter_context(tc.tile_pool(name="two", bufs=2))
        three = ctx.enter_context(tc.tile_pool(name="three", bufs=3))
        four = ctx.enter_context(tc.tile_pool(name="four", bufs=4))
        work_pool = ctx.enter_context(tc.psum_pool(name="work_pool", bufs=4))
        turned_pool = ctx.enter_context(tc.psum_pool(name="turned_pool", bufs=2))
        folded_pool = ctx.enter_context(tc.psum_pool(name="folded_pool", bufs=2))
        ctx.enter_context(tc.manual_schedule())

        lam_bf16 = keep.tile([P, 1], BF16, name="lam_bf16")
        lam_f32 = keep.tile([P, 1], F32, name="lam_f32")
        ident = keep.tile([P, P], F32, name="ident")
        fold_u = keep.tile([P, P], F32, name="fold_u")
        fold_v = keep.tile([P, P], F32, name="fold_v")
        table = keep.tile([P, 1], F32, name="table")
        p_t = keep.tile([P, PACK, ROWS], F32, name="p_t")
        th_t = keep.tile([P, PACK, ROWS], F32, name="th_t")
        sums = keep.tile([P, 2, PACK, ROWS], F32, name="sums")
        kappa_sb = keep.tile([P, PACK, K], BF16, name="kappa_sb", align_bytes=64)
        kappa_g = keep.tile([P, K, PACK], BF16, name="kappa_g", align_bytes=64)
        kappa_q = keep.tile([P, K], U32, name="kappa_q", align_bytes=64)
        kappa_s = keep.tile([P, K], U8, name="kappa_s", align_bytes=64)
        w_sb = keep.tile([P, 2, 4, K], BF16, name="w_sb", align_bytes=64)
        w_q = keep.tile([P, 2, C], U32, name="w_q", align_bytes=64)
        w_s = keep.tile([P, 2, C], U8, name="w_s", align_bytes=64)
        x_sb = keep.tile([P, T, PACK * C], BF16, name="x_sb", align_bytes=64)
        x_q = keep.tile([P, T, C], U32, name="x_q", align_bytes=64)
        x_s = keep.tile([P, T, C], U8, name="x_s", align_bytes=64)
        dp_g = keep.tile([P, K, PACK], BF16, name="dp_g", align_bytes=64)
        dp_q = keep.tile([P, K], U32, name="dp_q", align_bytes=64)
        dp_s = keep.tile([P, K], U8, name="dp_s", align_bytes=64)

        raw, banks, grads, mixed, dz2_q, dz2_s = {}, {}, {}, {}, {}, {}
        tanhs, squares, weighted, turned, turned_sb, folded = {}, {}, {}, {}, {}, {}
        w_g, x_g, dz1_g, dz1_q, dz1_s = {}, {}, {}, {}, {}

        def new_bank(key):
            bank = work_pool.tile([P, BANK], F32, name="bank")
            banks[key] = bank
            return bank

        def quantize(codes, scales, grouped, fmt):
            nc.vector.quantize_mx(
                out=codes.bitcast(fmt), scales=scales, in_=grouped[:].rearrange("p c t -> p (c t)")
            )

        def load_rows(r):
            for name, src in (("p", p), ("th", th)):
                tile = two.tile([P, K], F32, name="raw_" + name)
                raw[name, r] = tile
                nc.sync.dma_start(out=tile[:], in_=src.rearrange("b j c -> (b j) c")[r * P : (r + 1) * P, :])

        def turn_rows(name, r):
            bank = new_bank((name, r))
            for t in range(PACK):
                nc.tensor.transpose(bank[:, t * P : (t + 1) * P], raw[name, r][:, t:K:PACK], ident[:])

        def take_rows(name, r):
            src = banks[name, r][:].rearrange("p (t q) -> p t q", t=PACK)
            dst = (p_t if name == "p" else th_t)[:, :, r * P : (r + 1) * P]
            if (name, r) == ("th", 0):
                nc.scalar.copy(out=dst, in_=src)
            else:
                nc.vector.tensor_copy(out=dst, in_=src)

        def turn_weight(weight, half, key):
            bank = new_bank(key)
            for i in range(2):
                pairs_of_k = weight[:, 2 * half + i, :].bitcast(F32)
                for u in range(2):
                    col = (2 * i + u) * P
                    nc.tensor.transpose(bank[:, col : col + P], pairs_of_k[:, u : K // 2 : 2], ident[:])

        def take_weight(grouped, half, key):
            src = banks[key][:].rearrange("p (i u m) -> p i m u", i=2, u=2)
            flat = grouped[:].rearrange("p c t -> p (c t)").bitcast(F32)
            dst = flat[:, half * BANK : (half + 1) * BANK].rearrange("p (i m u) -> p i m u", i=2, u=2)
            nc.vector.tensor_copy(out=dst, in_=src)

        def load_grad(b):
            tile = three.tile([P, PACK, PAIRS], BF16, name="grad", align_bytes=64)
            grads[b] = tile
            nc.sync.dma_start(out=tile[:], in_=grad_out[b].rearrange("(p j) u v -> p j (u v)", j=PACK))

        def mix(b, half, engine):
            if half == 0:
                mixed[b] = keep.tile([P, PAIRS, PACK], BF16, name="mixed", align_bytes=64)
            cols = slice(half * BANK, (half + 1) * BANK)
            engine.tensor_scalar(
                out=mixed[b][:, cols, :], in0=grads[b][:, :, cols].rearrange("p j n -> p n j"),
                scalar1=lam_f32[:, 0:1], scalar2=0.0, op0=ALU.mult, op1=ALU.add,
            )

        def quantize_dz2(b, lo, hi):
            if lo == 0:
                dz2_q[b] = three.tile([P, PAIRS], U32, name="dz2_q", align_bytes=64)
                dz2_s[b] = three.tile([P, PAIRS], U8, name="dz2_s", align_bytes=64)
            cols = slice(lo, hi)
            quantize(dz2_q[b][:, cols], dz2_s[b][:, cols], mixed[b][:, cols, :], E5M2)

        def tanh(n):
            b, ct = divmod(n, PACK)
            tile = four.tile([P, PAIRS], F32, name="f")
            tanhs[n] = tile
            for u in range(V):
                row = b * V + u
                nc.scalar.activation(
                    out=tile[:, u * V : (u + 1) * V], in_=th_t[:, ct, b * V : (b + 1) * V], func=ACT.Tanh,
                    bias=p_t[:, ct, row : row + 1], scale=-1.0,
                )

        def on_gpsimd(n):
            return (n % PACK == GPSIMD_SQUARE_CT and n >= 2 * PACK - 1) or n in LATE_GPSIMD_UNITS

        def square(n):
            tile = four.tile([P, PAIRS], F32, name="f_squared")
            squares[n] = tile
            f = tanhs[n]
            if on_gpsimd(n):
                nc.gpsimd.tensor_tensor(out=tile[:], in0=f[:], in1=f[:], op=ALU.mult)
            elif n < VECTOR_SQUARES:
                nc.vector.tensor_tensor(out=tile[:], in0=f[:], in1=f[:], op=ALU.mult)
            else:
                nc.scalar.activation(out=tile[:], in_=f[:], func=ACT.Square)

        def multiply(n):
            b, ct = divmod(n, PACK)
            channels = slice(ct * P, (ct + 1) * P)
            for half in range(2):
                cols = slice(half * BANK, (half + 1) * BANK)
                bank = new_bank((n, half))
                nc.tensor.matmul_mx(
                    out=bank[:], lhsT=kappa_q[:, channels].bitcast(E4M3), lhsT_scale=kappa_s[:, channels],
                    rhs=dz2_q[b][:, cols].bitcast(E5M2), rhs_scale=dz2_s[b][:, cols], start=True, stop=True,
                )

        def weigh(n):
            tile = four.tile([P, PAIRS], F32, name="minus_ds")
            weighted[n] = tile
            for half in range(2):
                cols = slice(half * BANK, (half + 1) * BANK)
                nc.vector.scalar_tensor_tensor(
                    out=tile[:, cols], in0=squares[n][:, cols], scalar=1.0, in1=banks[n, half][:],
                    op0=ALU.subtract, op1=ALU.mult,
                )

        def tensor_sums_v(n):
            return n % PACK == TENSOR_SUM_CT and n < LAST_BATCH

        def sum_over_v(n):
            b, ct = divmod(n, PACK)
            nc.vector.tensor_reduce(
                out=sums[:, 0, ct, b * V : (b + 1) * V],
                in_=weighted[n][:].rearrange("p (u v) -> p u v", v=V), axis=AXIS.X, op=ALU.add,
            )

        def turn_sums(n):
            tile = turned_pool.tile([P, 2 * P], F32, name="turned")
            turned[n] = tile
            src = weighted[n]
            for i in range(BLOCKS):
                nc.tensor.matmul(
                    tile[:, 0:P], src[:, i * P : (i + 1) * P], ident[:],
                    start=(i == 0), stop=(i == BLOCKS - 1), is_transpose=True,
                )
            if tensor_sums_v(n):
                for r in range(BLOCKS):
                    nc.tensor.matmul(
                        tile[:, P : 2 * P], src[:, r:PAIRS:BLOCKS], ident[:],
                        start=(r == 0), stop=(r == BLOCKS - 1), is_transpose=True,
                    )

        def take_sums(n):
            tile = three.tile([P, 2 * P], F32, name="turned_sb")
            turned_sb[n] = tile
            cols = slice(0, 2 * P if tensor_sums_v(n) else P)
            if n >= SCALAR_TAKES_FROM:
                nc.scalar.copy(out=tile[:, cols], in_=turned[n][:, cols])
            else:
                nc.vector.tensor_copy(out=tile[:, cols], in_=turned[n][:, cols])

        def fold_sums(n):
            tile = folded_pool.tile([P, 2 * P], F32, name="folded")
            folded[n] = tile
            for i, matrix in enumerate((fold_u, fold_v) if tensor_sums_v(n) else (fold_u,)):
                cols = slice(i * P, (i + 1) * P)
                nc.tensor.matmul(tile[:, cols], turned_sb[n][:, cols], matrix[:], start=True, stop=True)

        def keep_sums(n):
            b, ct = divmod(n, PACK)
            rows = slice(b * V, (b + 1) * V)
            if tensor_sums_v(n):
                nc.vector.tensor_copy(out=sums[:, 0, ct, rows], in_=folded[n][:, P : P + V])
            if n >= LAST_BATCH:
                nc.scalar.copy(out=sums[:, 1, ct, rows], in_=folded[n][:, 0:V])
            else:
                nc.vector.tensor_copy(out=sums[:, 1, ct, rows], in_=folded[n][:, 0:V])

        def round_dz1(g, part):
            tile = two.tile([P, P, PACK], BF16, name="dz1_g%d" % part, align_bytes=64)
            dz1_g[g, part] = tile
            src = sums[:, part, :, g * P : (g + 1) * P].rearrange("p t n -> p n t")
            factor = (-0.25, 0.25)[part]
            if g == 3:
                nc.scalar.activation(out=tile[:], in_=src, func=ACT.Copy, scale=factor)
            else:
                nc.vector.tensor_scalar(out=tile[:], in0=src, scalar1=factor, scalar2=None, op0=ALU.mult)

        def quantize_dz1(g, part):
            dz1_q[g, part] = two.tile([P, P], U32, name="dz1_q%d" % part, align_bytes=64)
            dz1_s[g, part] = two.tile([P, P], U8, name="dz1_s%d" % part, align_bytes=64)
            quantize(dz1_q[g, part][:], dz1_s[g, part][:], dz1_g[g, part], E5M2)

        def multiply_out_0(g):
            bank = new_bank(("out_0", g))
            for part in range(2):
                nc.tensor.matmul_mx(
                    out=bank[:], lhsT=dz1_q[g, part][:].bitcast(E5M2), lhsT_scale=dz1_s[g, part][:],
                    rhs=w_q[:, part, :].bitcast(E4M3), rhs_scale=w_s[:, part, :],
                    start=(part == 0), stop=(part == 1),
                )

        def store_out_0(g):
            tile = two.tile([P, C], F32, name="out_0_rows")
            if g < 2:
                nc.vector.tensor_copy(out=tile[:], in_=banks["out_0", g][:])
            else:
                nc.scalar.copy(out=tile[:], in_=banks["out_0", g][:])
            for i in range(4):
                src = tile[i * V : (i + 1) * V, :].unsqueeze(1).to_broadcast([V, T, C])
                nc.sync.dma_start(out=out_0[4 * g + i].rearrange("t j c -> j t c"), in_=src)

        def load_weights():
            for i, w in enumerate((phi_w, theta_w)):
                nc.sync.dma_start(out=w_sb[:, i, :, :], in_=w.rearrange("(r m) k -> m r k", m=P))

        def turn_w(i, half):
            if half == 0:
                w_g[i] = two.tile([P, C, PACK], BF16, name="w_g", align_bytes=64)
            turn_weight(w_sb[:, i, :, :], half, ("w", i, half))

        def take_w(i, half):
            take_weight(w_g[i], half, ("w", i, half))

        def quantize_w(i):
            quantize(w_q[:, i, :], w_s[:, i, :], w_g[i], E4M3)

        def load_x(b):
            src = x[b].rearrange("t (q j) c -> q t (j c)", j=PACK)
            nc.sync.dma_start(out=x_sb[8 * b : 8 * b + 8, :, :], in_=src)

        def mix_x(t, half):
            if half == 0:
                x_g[t] = two.tile([P, C, PACK], BF16, name="x_g", align_bytes=64)
            cols = slice(half * C // 2, (half + 1) * C // 2)
            src = x_sb[:, t, :].rearrange("p (j c) -> p c j", j=PACK)
            nc.vector.tensor_copy(out=x_g[t][:, cols, :], in_=src[:, cols, :])

        def quantize_x(t):
            quantize(x_q[:, t, :], x_s[:, t, :], x_g[t], E4M3)

        def turn_dp(ct):
            bank = new_bank(("dp", ct))
            for t in range(PACK):
                nc.tensor.transpose(bank[:, t * P : (t + 1) * P], sums[:, 0, ct, t:ROWS:PACK], ident[:])

        def round_dp(ct):
            nc.scalar.activation(
                out=dp_g[:, ct * P : (ct + 1) * P, :],
                in_=banks["dp", ct][:].rearrange("p (t m) -> p m t", t=PACK), func=ACT.Copy, scale=-0.25,
            )

        def quantize_dp(ct):
            cols = slice(ct * P, (ct + 1) * P)
            quantize(dp_q[:, cols], dp_s[:, cols], dp_g[:, cols, :], E5M2)

        def out_1_rows(i):
            rows = slice(i * P, (i + 1) * P)
            bank = new_bank(("out_1", i))
            for t in range(T):
                nc.tensor.matmul_mx(
                    out=bank[:], lhsT=x_q[:, t, rows].bitcast(E4M3), lhsT_scale=x_s[:, t, rows],
                    rhs=dp_q[:].bitcast(E5M2), rhs_scale=dp_s[:], start=(t == 0), stop=(t == T - 1),
                )
            tile = four.tile([P, K], F32, name="out_1_rows")
            src = bank[:].rearrange("p (t m) -> p m t", t=PACK)
            dst = tile[:].rearrange("p (m t) -> p m t", t=PACK)
            if i % 2 == 0:
                nc.vector.tensor_copy(out=dst, in_=src)
            else:
                nc.scalar.copy(out=dst, in_=src)
            nc.sync.dma_start(out=out_1[rows, :], in_=tile[:])

        nc.scalar.dma_start(out=lam_bf16[:], in_=lam.partition_broadcast(P))
        load_rows(0)
        grads[0] = three.tile([P, PACK, PAIRS], BF16, name="grad", align_bytes=64)
        first_grad = grad_out[0].rearrange("(p j) u v -> p j (u v)", j=PACK)
        nc.sync.dma_start(out=grads[0][:, :, 0:BANK], in_=first_grad[:, :, 0:BANK])
        nc.sync.dma_start(out=kappa_sb[:], in_=kappa_w.rearrange("(m t) k -> m t k", t=PACK))
        nc.sync.dma_start(out=grads[0][:, :, BANK:PAIRS], in_=first_grad[:, :, BANK:PAIRS])
        load_grad(1)
        load_rows(1)
        load_grad(2)
        make_identity(nc, ident[:])
        nc.vector.memset(table[:], 0.0)
        nc.scalar.activation(out=table[:], in_=table[:], func=ACT.Tanh)
        for c in range(P // V):
            for matrix, pattern in ((fold_u, "p (a v) -> p v a"), (fold_v, "p (v a) -> p v a")):
                nc.vector.tensor_reduce(
                    out=matrix[:, c * V : (c + 1) * V], in_=ident[:].rearrange(pattern, v=V), axis=AXIS.X, op=ALU.add
                )
        turn_rows("p", 0)
        turn_rows("th", 0)
        take_rows("p", 0)
        take_rows("th", 0)
        turn_weight(kappa_sb, 0, ("kappa", 0))
        turn_weight(kappa_sb, 1, ("kappa", 1))
        nc.vector.tensor_copy(out=lam_f32[:], in_=lam_bf16[:])
        mix(0, 0, nc.vector)
        mix(0, 1, nc.gpsimd)
        tanh(0)
        take_weight(kappa_g, 0, ("kappa", 0))
        take_weight(kappa_g, 1, ("kappa", 1))
        quantize_dz2(0, 0, BANK)
        quantize(kappa_q[:], kappa_s[:], kappa_g, E4M3)
        quantize_dz2(0, BANK, PAIRS)
        square(0)
        tanh(1)
        square(1)
        tanh(2)
        tanh(3)
        mix(1, 0, nc.gpsimd)
        mix(1, 1, nc.gpsimd)
        multiply(0)

        beside = {}

        def at(step, function, *arguments):
            beside.setdefault(step, []).append((function, arguments))

        for r in range(1, 4):
            first = 16 * r - 12
            if r > 1:
                at(first - 10, load_rows, r)
            for i, name in enumerate(("p", "th")):
                at(first + 2 * i, turn_rows, name, r)
                at(first + 2 * i + 1, take_rows, name, r)
        at(0, load_weights)
        for i in range(2):
            first = 8 + 4 * i
            for half in range(2):
                at(first + 2 * half, turn_w, i, half)
                at(first + 2 * half + 1, take_w, i, half)
            at(first + 5, quantize_w, i)
        for b in range(B):
            at(9 + b, load_x, b)
        for t in range(T):
            for half in range(2):
                at(29 + 8 * t + 4 * half, mix_x, t, half)
            at(37 + 8 * t, quantize_x, t)
        for g in range(4):
            done = 16 * g + 12
            late = g == 3
            for part in range(2):
                at(done + (8 if late else 13), round_dz1, g, part)
                at(done + (9 if late else 17), quantize_dz1, g, part)
            at(done + (9 if late else 17), multiply_out_0, g)
            at(done + (10 if late else 18), store_out_0, g)
        for b in range(B):
            if 3 <= b + 2 < B:
                at(4 * b - 4, load_grad, b + 2)
            if b + 1 < B:
                at(4 * b + 1, quantize_dz2, b + 1, 0, PAIRS)
            if b + 2 < B:
                at(4 * b + 2, mix, b + 2, 0, nc.gpsimd)
                at(4 * b + 2, mix, b + 2, 1, nc.gpsimd)
        for n in range(UNITS):
            if on_gpsimd(n):
                at(n - 3, square, n)
        for n in range(UNITS):
            late = n >= LAST_BATCH
            at(n + (2 if late else 3), take_sums, n)
            at(n + (3 if late else 4), fold_sums, n)
            at(n + (4 if late else 5), keep_sums, n)
        for ct in range(PACK):
            at(LAST_BATCH + ct + 1, turn_dp, ct)
            at(LAST_BATCH + ct + 2, round_dp, ct)
            at(LAST_BATCH + ct + 3, quantize_dp, ct)
        for i in range(4):
            at(UNITS + 5 + i, out_1_rows, i)

        for s in range(UNITS + 10):
            if s + 4 < UNITS:
                tanh(s + 4)
            if s + 2 < UNITS and not on_gpsimd(s + 2):
                square(s + 2)
            if s + 1 < UNITS:
                multiply(s + 1)
            if s < UNITS:
                weigh(s)
            if 0 <= s - 1 < UNITS and not tensor_sums_v(s - 1):
                sum_over_v(s - 1)
            if 0 <= s - 2 < LAST_BATCH:
                turn_sums(s - 2)
            if LAST_BATCH <= s - 1 < UNITS:
                turn_sums(s - 1)
            for function, arguments in beside.get(s, []):
                function(*arguments)
